import numpy as np
import ml_dtypes


def mxq(x, axis, fmt="e4m3"):
    dtype, down = {"e4m3": (ml_dtypes.float8_e4m3fn, 7), "e5m2": (ml_dtypes.float8_e5m2, 14)}[fmt]
    v = np.moveaxis(np.asarray(x, np.float32).astype(ml_dtypes.bfloat16).astype(np.float64), axis, -1)
    blocks = v.reshape(v.shape[:-1] + (-1, 32))
    amax = np.abs(blocks).max(-1, keepdims=True)
    byte = np.maximum(np.where(amax > 0, np.frexp(amax)[1] - 1 + 127, 0) - down, 1)
    scale = np.exp2(byte - 127.0)
    codes = (blocks / scale).astype(np.float32).astype(dtype).astype(np.float64)
    return np.moveaxis((codes * scale).reshape(v.shape), -1, axis)


WIDE = False


def mx_kscale(k):
    if not WIDE:
        return np.ones(k)
    levels = np.array([10, -10, 5, -5, 0])
    a = np.random.permutation(np.resize(levels, k // 512 * 4)).reshape(k // 512, 4)
    idx = np.arange(k)
    return np.exp2(a[idx // 512, idx % 128 // 32])


BF16 = ml_dtypes.bfloat16


def bf(x):
    return np.asarray(x, np.float32).astype(BF16)


def f64(x):
    return np.asarray(x).astype(np.float64)


B, C, CQ, CV, H, W = 4, 512, 128, 256, 64, 64
P = H * W


def conv1x1(xq, w, b):
    y = (mxq(f64(w), 1, "e4m3") @ xq) + f64(b)[None, :, None]
    return y.reshape(B, w.shape[0], H, W)


def kronecker(y):
    return np.concatenate([y.mean(axis=3), y.mean(axis=2)], axis=2)


def setup_inputs():
    s = mx_kscale(C)
    g = 3.0 / np.sqrt(C)
    return {"x": bf(np.random.standard_normal((B, C, H, W)) * s[None, :, None, None]),
            "Wq": bf(np.random.standard_normal((CQ, C)) * g / s[None, :]),
            "bq": bf(np.random.standard_normal(CQ) * 0.1),
            "Wk": bf(np.random.standard_normal((CQ, C)) * g / s[None, :]),
            "bk": bf(np.random.standard_normal(CQ) * 0.1),
            "Wv": bf(np.random.standard_normal((CV, C)) * g / s[None, :]),
            "bv": bf(np.random.standard_normal(CV) * 0.1)}


def reference(x, Wq, bq, Wk, bk, Wv, bv):
    xq = mxq(f64(x).reshape(B, C, P), 1, "e4m3")
    q = kronecker(conv1x1(xq, Wq, bq))
    k = kronecker(conv1x1(xq, Wk, bk))
    v = kronecker(conv1x1(xq, Wv, bv))
    return q, k, v

@@ -1,0 +1,167 @@
+from contextlib import ExitStack
+
+import concourse.masks as masks
+import concourse.mybir as mybir
+
+F32 = mybir.dt.float32
+BF16 = mybir.dt.bfloat16
+I32 = mybir.dt.int32
+U32 = mybir.dt.uint32
+U8 = mybir.dt.uint8
+FP8X4 = mybir.dt.float8_e4m3fn_x4
+ADD = mybir.AluOpType.add
+MULT = mybir.AluOpType.mult
+X_AXIS = mybir.AxisListType.X
+
+P = 128
+PACK = 4
+B, C, H, W = 4, 512, 64, 64
+PIXELS = H * W
+O_TILES = 4
+assert C == P * PACK and H == W
+
+WINDOW = 256
+BAND = WINDOW // W
+BANDS = H // BAND
+STRIP = WINDOW // H
+STRIPS = W // STRIP
+
+CHUNK_ROWS = 8
+CHUNKS = H // CHUNK_ROWS
+CHUNK_PIXELS = CHUNK_ROWS * W
+VECTOR_EVERY = 4
+
+FLOPS = 2 * B * C * (O_TILES * P) * PIXELS
+
+
+def quantise_weights(nc, const, psum, identity, Wq, Wk, Wv):
+    w_rows = const.tile([P, O_TILES * C], BF16)
+    nc.scalar.dma_start(out=w_rows[:, 0:C], in_=Wq)
+    nc.scalar.dma_start(out=w_rows[:, C : 2 * C], in_=Wk)
+    nc.scalar.dma_start(
+        out=w_rows[:, 2 * C : 4 * C].rearrange("o (r c) -> o r c", r=2),
+        in_=Wv.rearrange("(r o) c -> o r c", r=2),
+    )
+    w_pairs = w_rows[:].bitcast(F32).rearrange("o (r p u) -> o r u p", r=O_TILES, u=2)
+    w_grouped = const.tile([P, O_TILES * P * PACK], BF16, align_bytes=64)
+    w_grouped_pairs = w_grouped[:].bitcast(F32).rearrange("p (r o u) -> p r o u", r=O_TILES, u=2)
+    for half in range(2):
+        turned = psum.tile([P, 2, 2, P], F32, tag="bank")
+        for r in range(2):
+            for u in range(2):
+                nc.tensor.transpose(turned[:, r, u, :], w_pairs[:, 2 * half + r, u, :], identity[:])
+        nc.scalar.copy(
+            out=w_grouped_pairs[:, 2 * half : 2 * half + 2],
+            in_=turned[:].rearrange("p r u o -> p r o u"),
+        )
+    w_codes = const.tile([P, O_TILES * P], U32, align_bytes=64)
+    w_scales = const.tile([P, O_TILES * P], U8, align_bytes=64)
+    nc.vector.quantize_mx(out=w_codes[:].bitcast(FP8X4), scales=w_scales[:], in_=w_grouped[:])
+    return w_codes, w_scales
+
+
+def bias_columns(nc, const, psum, identity, bq, bk, bv):
+    bias_rows = const.tile([P, P], BF16)
+    nc.vector.memset(bias_rows[:], 0.0)
+    nc.scalar.dma_start(out=bias_rows[0:1, :], in_=bq.rearrange("(r o) -> r o", r=1))
+    nc.scalar.dma_start(out=bias_rows[1:2, :], in_=bk.rearrange("(r o) -> r o", r=1))
+    nc.scalar.dma_start(out=bias_rows[2:4, :], in_=bv.rearrange("(r o) -> r o", r=2))
+    bias_rows_f32 = const.tile([P, P], F32)
+    nc.vector.tensor_copy(out=bias_rows_f32[:], in_=bias_rows[:])
+    turned = psum.tile([P, P], F32, tag="bank")
+    nc.tensor.transpose(turned[:], bias_rows_f32[:], identity[:])
+    bias = const.tile([P, O_TILES], F32)
+    nc.vector.tensor_copy(out=bias[:], in_=turned[:, 0:O_TILES])
+    return bias
+
+
+def tile_pam_module_pa_t_kernel(tc, x, Wq, bq, Wk, bk, Wv, bv, out_0, out_1, out_2):
+    nc = tc.nc
+    with ExitStack() as ctx:
+        const = ctx.enter_context(tc.tile_pool(name="const", bufs=1))
+        keep = ctx.enter_context(tc.tile_pool(name="keep", bufs=B))
+        raw_pool = ctx.enter_context(tc.tile_pool(name="raw", bufs=6))
+        grouped_pool = ctx.enter_context(tc.tile_pool(name="grouped", bufs=3))
+        small = ctx.enter_context(tc.tile_pool(name="small", bufs=2))
+        psum = ctx.enter_context(tc.psum_pool(name="psum", bufs=8))
+
+        identity = const.tile([P, P], F32)
+        masks.make_identity(nc, identity[:])
+        w_codes, w_scales = quantise_weights(nc, const, psum, identity, Wq, Wk, Wv)
+        bias = bias_columns(nc, const, psum, identity, bq, bk, bv)
+
+        x_channels = x.rearrange("n (p t) h w -> n p t (h w)", t=PACK)
+
+        def product(acc, r, codes, scales, window, first, last):
+            pixels = slice(window * WINDOW, (window + 1) * WINDOW)
+            outputs = slice(r * P, (r + 1) * P)
+            nc.tensor.matmul_mx(
+                out=acc[:],
+                lhsT=w_codes[:, outputs].bitcast(FP8X4),
+                lhsT_scale=w_scales[:, outputs],
+                rhs=codes[:, pixels].bitcast(FP8X4),
+                rhs_scale=scales[:, pixels],
+                start=first,
+                stop=last,
+            )
+
+        for n in range(B):
+            pooled_to = [out_0[n], out_1[n], out_2[n, 0:P], out_2[n, P : 2 * P]]
+            codes_by_row = keep.tile([P, PIXELS], U32, align_bytes=64)
+            scales_by_row = keep.tile([P, PIXELS], U8, align_bytes=64)
+            codes_by_strip = keep.tile([P, PIXELS], U32, align_bytes=64)
+            scales_by_strip = keep.tile([P, PIXELS], U8, align_bytes=64)
+            nc.vector.memset(scales_by_row[:].bitcast(I32), 0)
+
+            sums = small.tile([P, O_TILES, H + W], F32)
+            column_acc = [psum.tile([P, WINDOW], F32, name="column_acc", tag="bank") for r in range(O_TILES)]
+            for c in range(CHUNKS):
+                pixels = slice(c * CHUNK_PIXELS, (c + 1) * CHUNK_PIXELS)
+                rows = slice(c * CHUNK_ROWS, (c + 1) * CHUNK_ROWS)
+                raw = raw_pool.tile([P, PACK, CHUNK_PIXELS], BF16)
+                nc.sync.dma_start(out=raw[:], in_=x_channels[n, :, :, pixels])
+                grouped = grouped_pool.tile([P, CHUNK_PIXELS * PACK], BF16, align_bytes=64)
+                grouped_view = grouped[:].rearrange("p (q i t) -> p q t i", i=4, t=PACK)
+                raw_view = raw[:].rearrange("p t (q i) -> p q t i", i=4)
+                if (n * CHUNKS + c) % VECTOR_EVERY == 0:
+                    nc.vector.tensor_copy(out=grouped_view, in_=raw_view)
+                else:
+                    nc.scalar.copy(out=grouped_view, in_=raw_view)
+                nc.vector.quantize_mx(
+                    out=codes_by_row[:, pixels].bitcast(FP8X4),
+                    scales=scales_by_row[:, pixels],
+                    in_=grouped[:],
+                )
+                nc.vector.tensor_copy(
+                    out=codes_by_strip[:].bitcast(I32).rearrange("p (s i j) -> p s i j", s=STRIPS, j=STRIP)[:, :, rows, :],
+                    in_=codes_by_row[:].bitcast(I32).rearrange("p (i s j) -> p s i j", s=STRIPS, j=STRIP)[:, :, rows, :],
+                )
+                nc.vector.tensor_copy(
+                    out=scales_by_strip[:].bitcast(I32).rearrange("p (s i j) -> p s i j", s=STRIPS, j=STRIP // 4)[:, :, rows, :],
+                    in_=scales_by_row[:].bitcast(I32).rearrange("p (i s j) -> p s i j", s=STRIPS, j=STRIP // 4)[:, :, rows, :],
+                )
+                for band in range(c * CHUNK_ROWS // BAND, (c + 1) * CHUNK_ROWS // BAND):
+                    for r in range(O_TILES):
+                        product(column_acc[r], r, codes_by_row, scales_by_row, band, band == 0, band == BANDS - 1)
+            for r in range(O_TILES):
+                nc.vector.tensor_reduce(
+                    out=sums[:, r, H : H + W],
+                    in_=column_acc[r][:].rearrange("p (i j) -> p j i", i=BAND),
+                    axis=X_AXIS,
+                    op=ADD,
+                )
+            for r in range(O_TILES):
+                row_acc = psum.tile([P, WINDOW], F32, tag="bank")
+                for strip in range(STRIPS):
+                    product(row_acc, r, codes_by_strip, scales_by_strip, strip, strip == 0, strip == STRIPS - 1)
+                nc.vector.tensor_reduce(
+                    out=sums[:, r, 0:H],
+                    in_=row_acc[:].rearrange("p (i j) -> p i j", j=STRIP),
+                    axis=X_AXIS,
+                    op=ADD,
+                )
+                pooled = small.tile([P, H + W], F32)
+                nc.vector.tensor_scalar(
+                    out=pooled[:], in0=sums[:, r, :], scalar1=1.0 / W, scalar2=bias[:, r : r + 1], op0=MULT, op1=ADD
+                )
+                nc.sync.dma_start(out=pooled_to[r], in_=pooled[:])

@@ -20,14 +20,16 @@ PIXELS = H * W
 O_TILES = 4
 assert C == P * PACK and H == W
 
-WINDOW = 256
+WINDOW = 512
 BAND = WINDOW // W
 BANDS = H // BAND
-STRIP = WINDOW // H
+BLOCK_ROWS = 64
+BLOCKS = H // BLOCK_ROWS
+STRIP = WINDOW // BLOCK_ROWS
 STRIPS = W // STRIP
 
 CHUNK_ROWS = 8
-CHUNKS = H // CHUNK_ROWS
+CHUNKS = BLOCK_ROWS // CHUNK_ROWS
 CHUNK_PIXELS = CHUNK_ROWS * W
 VECTOR_EVERY = 4
 
@@ -83,7 +85,8 @@ def tile_pam_module_pa_t_kernel(tc, x, Wq, bq, Wk, bk, Wv, bv, out_0, out_1, out
         raw_pool = ctx.enter_context(tc.tile_pool(name="raw", bufs=6))
         grouped_pool = ctx.enter_context(tc.tile_pool(name="grouped", bufs=3))
         small = ctx.enter_context(tc.tile_pool(name="small", bufs=2))
-        psum = ctx.enter_context(tc.psum_pool(name="psum", bufs=8))
+        column_psum = ctx.enter_context(tc.psum_pool(name="column_psum", bufs=O_TILES))
+        psum = ctx.enter_context(tc.psum_pool(name="psum", bufs=8 - O_TILES))
 
         identity = const.tile([P, P], F32)
         masks.make_identity(nc, identity[:])
@@ -94,11 +97,10 @@ def tile_pam_module_pa_t_kernel(tc, x, Wq, bq, Wk, bk, Wv, bv, out_0, out_1, out
 
         def product(acc, r, codes, scales, window, first, last):
             pixels = slice(window * WINDOW, (window + 1) * WINDOW)
-            outputs = slice(r * P, (r + 1) * P)
             nc.tensor.matmul_mx(
                 out=acc[:],
-                lhsT=w_codes[:, outputs].bitcast(FP8X4),
-                lhsT_scale=w_scales[:, outputs],
+                lhsT=w_codes[:, r * P : (r + 1) * P].bitcast(FP8X4),
+                lhsT_scale=w_scales[:, r * P : (r + 1) * P],
                 rhs=codes[:, pixels].bitcast(FP8X4),
                 rhs_scale=scales[:, pixels],
                 start=first,
@@ -114,49 +116,56 @@ def tile_pam_module_pa_t_kernel(tc, x, Wq, bq, Wk, bk, Wv, bv, out_0, out_1, out
             nc.vector.memset(scales_by_row[:].bitcast(I32), 0)
 
             sums = small.tile([P, O_TILES, H + W], F32)
-            column_acc = [psum.tile([P, WINDOW], F32, name="column_acc", tag="bank") for r in range(O_TILES)]
-            for c in range(CHUNKS):
-                pixels = slice(c * CHUNK_PIXELS, (c + 1) * CHUNK_PIXELS)
-                rows = slice(c * CHUNK_ROWS, (c + 1) * CHUNK_ROWS)
-                raw = raw_pool.tile([P, PACK, CHUNK_PIXELS], BF16)
-                nc.sync.dma_start(out=raw[:], in_=x_channels[n, :, :, pixels])
-                grouped = grouped_pool.tile([P, CHUNK_PIXELS * PACK], BF16, align_bytes=64)
-                grouped_view = grouped[:].rearrange("p (q i t) -> p q t i", i=4, t=PACK)
-                raw_view = raw[:].rearrange("p t (q i) -> p q t i", i=4)
-                if (n * CHUNKS + c) % VECTOR_EVERY == 0:
-                    nc.vector.tensor_copy(out=grouped_view, in_=raw_view)
-                else:
-                    nc.scalar.copy(out=grouped_view, in_=raw_view)
-                nc.vector.quantize_mx(
-                    out=codes_by_row[:, pixels].bitcast(FP8X4),
-                    scales=scales_by_row[:, pixels],
-                    in_=grouped[:],
-                )
-                nc.vector.tensor_copy(
-                    out=codes_by_strip[:].bitcast(I32).rearrange("p (s i j) -> p s i j", s=STRIPS, j=STRIP)[:, :, rows, :],
-                    in_=codes_by_row[:].bitcast(I32).rearrange("p (i s j) -> p s i j", s=STRIPS, j=STRIP)[:, :, rows, :],
-                )
-                nc.vector.tensor_copy(
-                    out=scales_by_strip[:].bitcast(I32).rearrange("p (s i j) -> p s i j", s=STRIPS, j=STRIP // 4)[:, :, rows, :],
-                    in_=scales_by_row[:].bitcast(I32).rearrange("p (i s j) -> p s i j", s=STRIPS, j=STRIP // 4)[:, :, rows, :],
-                )
-                for band in range(c * CHUNK_ROWS // BAND, (c + 1) * CHUNK_ROWS // BAND):
-                    for r in range(O_TILES):
-                        product(column_acc[r], r, codes_by_row, scales_by_row, band, band == 0, band == BANDS - 1)
+            column_acc = [column_psum.tile([P, WINDOW], F32, name="column_acc", tag="bank") for r in range(O_TILES)]
+            for block in range(BLOCKS):
+                for c in range(CHUNKS):
+                    first_row = block * BLOCK_ROWS + c * CHUNK_ROWS
+                    pixels = slice(first_row * W, (first_row + CHUNK_ROWS) * W)
+                    rows = slice(c * CHUNK_ROWS, (c + 1) * CHUNK_ROWS)
+                    raw = raw_pool.tile([P, PACK, CHUNK_PIXELS], BF16)
+                    nc.sync.dma_start(out=raw[:], in_=x_channels[n, :, :, pixels])
+                    grouped = grouped_pool.tile([P, CHUNK_PIXELS * PACK], BF16, align_bytes=64)
+                    grouped_view = grouped[:].rearrange("p (q i t) -> p q t i", i=4, t=PACK)
+                    raw_view = raw[:].rearrange("p t (q i) -> p q t i", i=4)
+                    if ((n * BLOCKS + block) * CHUNKS + c) % VECTOR_EVERY == 0:
+                        nc.vector.tensor_copy(out=grouped_view, in_=raw_view)
+                    else:
+                        nc.scalar.copy(out=grouped_view, in_=raw_view)
+                    nc.vector.quantize_mx(
+                        out=codes_by_row[:, pixels].bitcast(FP8X4),
+                        scales=scales_by_row[:, pixels],
+                        in_=grouped[:],
+                    )
+                    nc.vector.tensor_copy(
+                        out=codes_by_strip[:].bitcast(I32).rearrange(
+                            "p (b s i j) -> p b s i j", b=BLOCKS, s=STRIPS, j=STRIP)[:, block, :, rows, :],
+                        in_=codes_by_row[:].bitcast(I32).rearrange(
+                            "p (b i s j) -> p b s i j", b=BLOCKS, s=STRIPS, j=STRIP)[:, block, :, rows, :],
+                    )
+                    nc.vector.tensor_copy(
+                        out=scales_by_strip[:].bitcast(I32).rearrange(
+                            "p (b s i j) -> p b s i j", b=BLOCKS, s=STRIPS, j=STRIP // 4)[:, block, :, rows, :],
+                        in_=scales_by_row[:].bitcast(I32).rearrange(
+                            "p (b i s j) -> p b s i j", b=BLOCKS, s=STRIPS, j=STRIP // 4)[:, block, :, rows, :],
+                    )
+                    for band in range(first_row // BAND, (first_row + CHUNK_ROWS) // BAND):
+                        for r in range(O_TILES):
+                            product(column_acc[r], r, codes_by_row, scales_by_row, band, band == 0, band == BANDS - 1)
+                for r in range(O_TILES):
+                    row_acc = psum.tile([P, WINDOW], F32, tag="bank")
+                    for strip in range(STRIPS):
+                        product(row_acc, r, codes_by_strip, scales_by_strip, block * STRIPS + strip,
+                                strip == 0, strip == STRIPS - 1)
+                    nc.vector.tensor_reduce(
+                        out=sums[:, r, block * BLOCK_ROWS : (block + 1) * BLOCK_ROWS],
+                        in_=row_acc[:].rearrange("p (i j) -> p i j", j=STRIP),
+                        axis=X_AXIS,
+                        op=ADD,
+                    )
             for r in range(O_TILES):
                 nc.vector.tensor_reduce(
                     out=sums[:, r, H : H + W],
                     in_=column_acc[r][:].rearrange("p (i j) -> p j i", i=BAND),
-                    axis=X_AXIS,
-                    op=ADD,
-                )
-            for r in range(O_TILES):
-                row_acc = psum.tile([P, WINDOW], F32, tag="bank")
-                for strip in range(STRIPS):
-                    product(row_acc, r, codes_by_strip, scales_by_strip, strip, strip == 0, strip == STRIPS - 1)
-                nc.vector.tensor_reduce(
-                    out=sums[:, r, 0:H],
-                    in_=row_acc[:].rearrange("p (i j) -> p i j", j=STRIP),
                     axis=X_AXIS,
                     op=ADD,
                 )

@@ -33,6 +33,7 @@ CHUNKS = BLOCK_ROWS // CHUNK_ROWS
 CHUNK_PIXELS = CHUNK_ROWS * W
 VECTOR_EVERY = 4
 
+W_PAD = 48
 FLOPS = 2 * B * C * (O_TILES * P) * PIXELS
 
 
@@ -56,9 +57,14 @@ def quantise_weights(nc, const, psum, identity, Wq, Wk, Wv):
             out=w_grouped_pairs[:, 2 * half : 2 * half + 2],
             in_=turned[:].rearrange("p r u o -> p r o u"),
         )
-    w_codes = const.tile([P, O_TILES * P], U32, align_bytes=64)
-    w_scales = const.tile([P, O_TILES * P], U8, align_bytes=64)
-    nc.vector.quantize_mx(out=w_codes[:].bitcast(FP8X4), scales=w_scales[:], in_=w_grouped[:])
+    w_codes = const.tile([P, W_PAD + O_TILES * P], U32, align_bytes=256)
+    w_scales = const.tile([P, O_TILES * 2 * P], U8, align_bytes=256)
+    for r in range(O_TILES):
+        nc.vector.quantize_mx(
+            out=w_codes[:, W_PAD + r * P : W_PAD + (r + 1) * P].bitcast(FP8X4),
+            scales=w_scales[:, 2 * r * P : (2 * r + 1) * P],
+            in_=w_grouped[:, r * P * PACK : (r + 1) * P * PACK],
+        )
     return w_codes, w_scales
 
 
@@ -99,8 +105,8 @@ def tile_pam_module_pa_t_kernel(tc, x, Wq, bq, Wk, bk, Wv, bv, out_0, out_1, out
             pixels = slice(window * WINDOW, (window + 1) * WINDOW)
             nc.tensor.matmul_mx(
                 out=acc[:],
-                lhsT=w_codes[:, r * P : (r + 1) * P].bitcast(FP8X4),
-                lhsT_scale=w_scales[:, r * P : (r + 1) * P],
+                lhsT=w_codes[:, W_PAD + r * P : W_PAD + (r + 1) * P].bitcast(FP8X4),
+                lhsT_scale=w_scales[:, 2 * r * P : (2 * r + 1) * P],
                 rhs=codes[:, pixels].bitcast(FP8X4),
                 rhs_scale=scales[:, pixels],
                 start=first,
@@ -109,10 +115,10 @@ def tile_pam_module_pa_t_kernel(tc, x, Wq, bq, Wk, bk, Wv, bv, out_0, out_1, out
 
         for n in range(B):
             pooled_to = [out_0[n], out_1[n], out_2[n, 0:P], out_2[n, P : 2 * P]]
-            codes_by_row = keep.tile([P, PIXELS], U32, align_bytes=64)
-            scales_by_row = keep.tile([P, PIXELS], U8, align_bytes=64)
-            codes_by_strip = keep.tile([P, PIXELS], U32, align_bytes=64)
-            scales_by_strip = keep.tile([P, PIXELS], U8, align_bytes=64)
+            codes_by_row = keep.tile([P, PIXELS], U32, align_bytes=256)
+            scales_by_row = keep.tile([P, PIXELS], U8, align_bytes=256)
+            codes_by_strip = keep.tile([P, PIXELS], U32, align_bytes=256)
+            scales_by_strip = keep.tile([P, PIXELS], U8, align_bytes=256)
             nc.vector.memset(scales_by_row[:].bitcast(I32), 0)
 
             sums = small.tile([P, O_TILES, H + W], F32)

@@ -20,67 +20,24 @@ PIXELS = H * W
 O_TILES = 4
 assert C == P * PACK and H == W
 
-WINDOW = 512
+WINDOW = 256
 BAND = WINDOW // W
-BANDS = H // BAND
-BLOCK_ROWS = 64
+BLOCK_ROWS = 32
 BLOCKS = H // BLOCK_ROWS
+BLOCK_PIXELS = BLOCK_ROWS * W
+BANDS = BLOCK_ROWS // BAND
 STRIP = WINDOW // BLOCK_ROWS
 STRIPS = W // STRIP
 
 CHUNK_ROWS = 8
 CHUNKS = BLOCK_ROWS // CHUNK_ROWS
 CHUNK_PIXELS = CHUNK_ROWS * W
-VECTOR_EVERY = 4
+VECTOR_CHUNK = 1
 
 W_PAD = 48
+W_SLOT = 256
+
 FLOPS = 2 * B * C * (O_TILES * P) * PIXELS
-
-
-def quantise_weights(nc, const, psum, identity, Wq, Wk, Wv):
-    w_rows = const.tile([P, O_TILES * C], BF16)
-    nc.scalar.dma_start(out=w_rows[:, 0:C], in_=Wq)
-    nc.scalar.dma_start(out=w_rows[:, C : 2 * C], in_=Wk)
-    nc.scalar.dma_start(
-        out=w_rows[:, 2 * C : 4 * C].rearrange("o (r c) -> o r c", r=2),
-        in_=Wv.rearrange("(r o) c -> o r c", r=2),
-    )
-    w_pairs = w_rows[:].bitcast(F32).rearrange("o (r p u) -> o r u p", r=O_TILES, u=2)
-    w_grouped = const.tile([P, O_TILES * P * PACK], BF16, align_bytes=64)
-    w_grouped_pairs = w_grouped[:].bitcast(F32).rearrange("p (r o u) -> p r o u", r=O_TILES, u=2)
-    for half in range(2):
-        turned = psum.tile([P, 2, 2, P], F32, tag="bank")
-        for r in range(2):
-            for u in range(2):
-                nc.tensor.transpose(turned[:, r, u, :], w_pairs[:, 2 * half + r, u, :], identity[:])
-        nc.scalar.copy(
-            out=w_grouped_pairs[:, 2 * half : 2 * half + 2],
-            in_=turned[:].rearrange("p r u o -> p r o u"),
-        )
-    w_codes = const.tile([P, W_PAD + O_TILES * P], U32, align_bytes=256)
-    w_scales = const.tile([P, O_TILES * 2 * P], U8, align_bytes=256)
-    for r in range(O_TILES):
-        nc.vector.quantize_mx(
-            out=w_codes[:, W_PAD + r * P : W_PAD + (r + 1) * P].bitcast(FP8X4),
-            scales=w_scales[:, 2 * r * P : (2 * r + 1) * P],
-            in_=w_grouped[:, r * P * PACK : (r + 1) * P * PACK],
-        )
-    return w_codes, w_scales
-
-
-def bias_columns(nc, const, psum, identity, bq, bk, bv):
-    bias_rows = const.tile([P, P], BF16)
-    nc.vector.memset(bias_rows[:], 0.0)
-    nc.scalar.dma_start(out=bias_rows[0:1, :], in_=bq.rearrange("(r o) -> r o", r=1))
-    nc.scalar.dma_start(out=bias_rows[1:2, :], in_=bk.rearrange("(r o) -> r o", r=1))
-    nc.scalar.dma_start(out=bias_rows[2:4, :], in_=bv.rearrange("(r o) -> r o", r=2))
-    bias_rows_f32 = const.tile([P, P], F32)
-    nc.vector.tensor_copy(out=bias_rows_f32[:], in_=bias_rows[:])
-    turned = psum.tile([P, P], F32, tag="bank")
-    nc.tensor.transpose(turned[:], bias_rows_f32[:], identity[:])
-    bias = const.tile([P, O_TILES], F32)
-    nc.vector.tensor_copy(out=bias[:], in_=turned[:, 0:O_TILES])
-    return bias
 
 
 def tile_pam_module_pa_t_kernel(tc, x, Wq, bq, Wk, bk, Wv, bv, out_0, out_1, out_2):
@@ -88,95 +45,166 @@ def tile_pam_module_pa_t_kernel(tc, x, Wq, bq, Wk, bk, Wv, bv, out_0, out_1, out
     with ExitStack() as ctx:
         const = ctx.enter_context(tc.tile_pool(name="const", bufs=1))
         keep = ctx.enter_context(tc.tile_pool(name="keep", bufs=B))
-        raw_pool = ctx.enter_context(tc.tile_pool(name="raw", bufs=6))
-        grouped_pool = ctx.enter_context(tc.tile_pool(name="grouped", bufs=3))
+        raw_pool = ctx.enter_context(tc.tile_pool(name="raw", bufs=2 * CHUNKS))
+        grouped_pool = ctx.enter_context(tc.tile_pool(name="grouped", bufs=CHUNKS))
         small = ctx.enter_context(tc.tile_pool(name="small", bufs=2))
         column_psum = ctx.enter_context(tc.psum_pool(name="column_psum", bufs=O_TILES))
         psum = ctx.enter_context(tc.psum_pool(name="psum", bufs=8 - O_TILES))
-
-        identity = const.tile([P, P], F32)
-        masks.make_identity(nc, identity[:])
-        w_codes, w_scales = quantise_weights(nc, const, psum, identity, Wq, Wk, Wv)
-        bias = bias_columns(nc, const, psum, identity, bq, bk, bv)
+        ctx.enter_context(tc.manual_schedule())
 
         x_channels = x.rearrange("n (p t) h w -> n p t (h w)", t=PACK)
+        raw_chunks = {}
+        quantised = {}
+        pooling = {}
+
+        def load(k):
+            n, block = divmod(k, BLOCKS)
+            raw_chunks[k] = []
+            for c in range(CHUNKS):
+                first = block * BLOCK_PIXELS + c * CHUNK_PIXELS
+                raw = raw_pool.tile([P, PACK, CHUNK_PIXELS], BF16, name="raw")
+                nc.sync.dma_start(out=raw[:], in_=x_channels[n, :, :, first : first + CHUNK_PIXELS])
+                raw_chunks[k].append(raw)
+
+        def quantise(k):
+            n, block = divmod(k, BLOCKS)
+            codes_by_row, scales_by_row, codes_by_strip, scales_by_strip = quantised[n]
+            for c in range(CHUNKS):
+                first = block * BLOCK_PIXELS + c * CHUNK_PIXELS
+                grouped = grouped_pool.tile([P, CHUNK_PIXELS * PACK], BF16, align_bytes=64)
+                grouped_view = grouped[:].rearrange("p (q i t) -> p q t i", i=4, t=PACK)
+                raw_view = raw_chunks[k][c][:].rearrange("p t (q i) -> p q t i", i=4)
+                if c == VECTOR_CHUNK:
+                    nc.vector.tensor_copy(out=grouped_view, in_=raw_view)
+                else:
+                    nc.scalar.copy(out=grouped_view, in_=raw_view)
+                nc.vector.quantize_mx(
+                    out=codes_by_row[:, first : first + CHUNK_PIXELS].bitcast(FP8X4),
+                    scales=scales_by_row[:, first : first + CHUNK_PIXELS],
+                    in_=grouped[:],
+                )
+            pixels = slice(block * BLOCK_PIXELS, (block + 1) * BLOCK_PIXELS)
+            nc.vector.tensor_copy(
+                out=codes_by_strip[:, pixels].bitcast(I32).rearrange("p (s i j) -> p s i j", s=STRIPS, j=STRIP),
+                in_=codes_by_row[:, pixels].bitcast(I32).rearrange("p (i s j) -> p s i j", s=STRIPS, j=STRIP),
+            )
+            nc.vector.tensor_copy(
+                out=scales_by_strip[:, pixels].bitcast(I32).rearrange("p (s i j) -> p s i j", s=STRIPS, j=STRIP // 4),
+                in_=scales_by_row[:, pixels].bitcast(I32).rearrange("p (i s j) -> p s i j", s=STRIPS, j=STRIP // 4),
+            )
 
         def product(acc, r, codes, scales, window, first, last):
             pixels = slice(window * WINDOW, (window + 1) * WINDOW)
             nc.tensor.matmul_mx(
                 out=acc[:],
                 lhsT=w_codes[:, W_PAD + r * P : W_PAD + (r + 1) * P].bitcast(FP8X4),
-                lhsT_scale=w_scales[:, 2 * r * P : (2 * r + 1) * P],
+                lhsT_scale=w_scales[:, r * W_SLOT : r * W_SLOT + P],
                 rhs=codes[:, pixels].bitcast(FP8X4),
                 rhs_scale=scales[:, pixels],
                 start=first,
                 stop=last,
             )
 
-        for n in range(B):
+        def multiply_and_pool(k):
+            n, block = divmod(k, BLOCKS)
+            codes_by_row, scales_by_row, codes_by_strip, scales_by_strip = quantised[n]
+            if block == 0:
+                sums = small.tile([P, O_TILES, H + W], F32)
+                column_acc = [column_psum.tile([P, WINDOW], F32, name="column_acc", tag="bank") for r in range(O_TILES)]
+                pooling[n] = (sums, column_acc)
+            sums, column_acc = pooling[n]
+            last_block = block == BLOCKS - 1
+            for band in range(BANDS):
+                for r in range(O_TILES):
+                    product(column_acc[r], r, codes_by_row, scales_by_row, block * BANDS + band,
+                            block == 0 and band == 0, last_block and band == BANDS - 1)
+            if last_block:
+                for r in range(O_TILES):
+                    nc.vector.tensor_reduce(
+                        out=sums[:, r, H : H + W],
+                        in_=column_acc[r][:].rearrange("p (i j) -> p j i", i=BAND),
+                        axis=X_AXIS,
+                        op=ADD,
+                    )
             pooled_to = [out_0[n], out_1[n], out_2[n, 0:P], out_2[n, P : 2 * P]]
+            for r in range(O_TILES):
+                row_acc = psum.tile([P, WINDOW], F32, tag="bank")
+                for strip in range(STRIPS):
+                    product(row_acc, r, codes_by_strip, scales_by_strip, block * STRIPS + strip,
+                            strip == 0, strip == STRIPS - 1)
+                nc.vector.tensor_reduce(
+                    out=sums[:, r, block * BLOCK_ROWS : (block + 1) * BLOCK_ROWS],
+                    in_=row_acc[:].rearrange("p (i j) -> p i j", j=STRIP),
+                    axis=X_AXIS,
+                    op=ADD,
+                )
+                if last_block:
+                    pooled = small.tile([P, H + W], F32)
+                    nc.vector.tensor_scalar(
+                        out=pooled[:], in0=sums[:, r, :], scalar1=1.0 / W, scalar2=bias[:, r : r + 1],
+                        op0=MULT, op1=ADD,
+                    )
+                    nc.sync.dma_start(out=pooled_to[r], in_=pooled[:])
+
+        for n in range(B):
             codes_by_row = keep.tile([P, PIXELS], U32, align_bytes=256)
             scales_by_row = keep.tile([P, PIXELS], U8, align_bytes=256)
             codes_by_strip = keep.tile([P, PIXELS], U32, align_bytes=256)
             scales_by_strip = keep.tile([P, PIXELS], U8, align_bytes=256)
             nc.vector.memset(scales_by_row[:].bitcast(I32), 0)
+            quantised[n] = (codes_by_row, scales_by_row, codes_by_strip, scales_by_strip)
 
-            sums = small.tile([P, O_TILES, H + W], F32)
-            column_acc = [column_psum.tile([P, WINDOW], F32, name="column_acc", tag="bank") for r in range(O_TILES)]
-            for block in range(BLOCKS):
-                for c in range(CHUNKS):
-                    first_row = block * BLOCK_ROWS + c * CHUNK_ROWS
-                    pixels = slice(first_row * W, (first_row + CHUNK_ROWS) * W)
-                    rows = slice(c * CHUNK_ROWS, (c + 1) * CHUNK_ROWS)
-                    raw = raw_pool.tile([P, PACK, CHUNK_PIXELS], BF16)
-                    nc.sync.dma_start(out=raw[:], in_=x_channels[n, :, :, pixels])
-                    grouped = grouped_pool.tile([P, CHUNK_PIXELS * PACK], BF16, align_bytes=64)
-                    grouped_view = grouped[:].rearrange("p (q i t) -> p q t i", i=4, t=PACK)
-                    raw_view = raw[:].rearrange("p t (q i) -> p q t i", i=4)
-                    if ((n * BLOCKS + block) * CHUNKS + c) % VECTOR_EVERY == 0:
-                        nc.vector.tensor_copy(out=grouped_view, in_=raw_view)
-                    else:
-                        nc.scalar.copy(out=grouped_view, in_=raw_view)
-                    nc.vector.quantize_mx(
-                        out=codes_by_row[:, pixels].bitcast(FP8X4),
-                        scales=scales_by_row[:, pixels],
-                        in_=grouped[:],
-                    )
-                    nc.vector.tensor_copy(
-                        out=codes_by_strip[:].bitcast(I32).rearrange(
-                            "p (b s i j) -> p b s i j", b=BLOCKS, s=STRIPS, j=STRIP)[:, block, :, rows, :],
-                        in_=codes_by_row[:].bitcast(I32).rearrange(
-                            "p (b i s j) -> p b s i j", b=BLOCKS, s=STRIPS, j=STRIP)[:, block, :, rows, :],
-                    )
-                    nc.vector.tensor_copy(
-                        out=scales_by_strip[:].bitcast(I32).rearrange(
-                            "p (b s i j) -> p b s i j", b=BLOCKS, s=STRIPS, j=STRIP // 4)[:, block, :, rows, :],
-                        in_=scales_by_row[:].bitcast(I32).rearrange(
-                            "p (b i s j) -> p b s i j", b=BLOCKS, s=STRIPS, j=STRIP // 4)[:, block, :, rows, :],
-                    )
-                    for band in range(first_row // BAND, (first_row + CHUNK_ROWS) // BAND):
-                        for r in range(O_TILES):
-                            product(column_acc[r], r, codes_by_row, scales_by_row, band, band == 0, band == BANDS - 1)
-                for r in range(O_TILES):
-                    row_acc = psum.tile([P, WINDOW], F32, tag="bank")
-                    for strip in range(STRIPS):
-                        product(row_acc, r, codes_by_strip, scales_by_strip, block * STRIPS + strip,
-                                strip == 0, strip == STRIPS - 1)
-                    nc.vector.tensor_reduce(
-                        out=sums[:, r, block * BLOCK_ROWS : (block + 1) * BLOCK_ROWS],
-                        in_=row_acc[:].rearrange("p (i j) -> p i j", j=STRIP),
-                        axis=X_AXIS,
-                        op=ADD,
-                    )
-            for r in range(O_TILES):
-                nc.vector.tensor_reduce(
-                    out=sums[:, r, H : H + W],
-                    in_=column_acc[r][:].rearrange("p (i j) -> p j i", i=BAND),
-                    axis=X_AXIS,
-                    op=ADD,
-                )
-                pooled = small.tile([P, H + W], F32)
-                nc.vector.tensor_scalar(
-                    out=pooled[:], in0=sums[:, r, :], scalar1=1.0 / W, scalar2=bias[:, r : r + 1], op0=MULT, op1=ADD
-                )
-                nc.sync.dma_start(out=pooled_to[r], in_=pooled[:])
+        bias_rows = const.tile([P, P], BF16)
+        nc.gpsimd.memset(bias_rows[:], 0.0)
+        nc.scalar.dma_start(out=bias_rows[0:1, :], in_=bq.rearrange("(r o) -> r o", r=1))
+        nc.scalar.dma_start(out=bias_rows[1:2, :], in_=bk.rearrange("(r o) -> r o", r=1))
+        nc.scalar.dma_start(out=bias_rows[2:4, :], in_=bv.rearrange("(r o) -> r o", r=2))
+        identity = const.tile([P, P], F32)
+        masks.make_identity(nc, identity[:])
+        bias_rows_f32 = const.tile([P, P], F32)
+        nc.gpsimd.tensor_copy(out=bias_rows_f32[:], in_=bias_rows[:])
+
+        w_rows = const.tile([P, O_TILES * C], BF16)
+        nc.sync.dma_start(out=w_rows[:, 0:C], in_=Wq)
+        nc.sync.dma_start(out=w_rows[:, C : 2 * C], in_=Wk)
+        nc.sync.dma_start(
+            out=w_rows[:, 2 * C : 4 * C].rearrange("o (r c) -> o r c", r=2),
+            in_=Wv.rearrange("(r o) c -> o r c", r=2),
+        )
+        load(0)
+        load(1)
+
+        w_pairs = w_rows[:].bitcast(F32).rearrange("o (r p u) -> o r u p", r=O_TILES, u=2)
+        w_grouped = const.tile([P, O_TILES * P * PACK], BF16, align_bytes=64)
+        w_grouped_pairs = w_grouped[:].bitcast(F32).rearrange("p (r o u) -> p r o u", r=O_TILES, u=2)
+        for half in range(2):
+            turned = psum.tile([P, 2, 2, P], F32, tag="bank")
+            for r in range(2):
+                for u in range(2):
+                    nc.tensor.transpose(turned[:, r, u, :], w_pairs[:, 2 * half + r, u, :], identity[:])
+            nc.vector.tensor_copy(
+                out=w_grouped_pairs[:, 2 * half : 2 * half + 2],
+                in_=turned[:].rearrange("p r u o -> p r o u"),
+            )
+        w_codes = const.tile([P, W_PAD + O_TILES * P], U32, align_bytes=256)
+        w_scales = const.tile([P, O_TILES * W_SLOT], U8, align_bytes=256)
+        for r in range(O_TILES):
+            nc.vector.quantize_mx(
+                out=w_codes[:, W_PAD + r * P : W_PAD + (r + 1) * P].bitcast(FP8X4),
+                scales=w_scales[:, r * W_SLOT : r * W_SLOT + P],
+                in_=w_grouped[:, r * P * PACK : (r + 1) * P * PACK],
+            )
+
+        quantise(0)
+
+        bias_turned = psum.tile([P, P], F32, tag="bank")
+        nc.tensor.transpose(bias_turned[:], bias_rows_f32[:], identity[:])
+        bias = const.tile([P, O_TILES], F32)
+        nc.vector.tensor_copy(out=bias[:], in_=bias_turned[:, 0:O_TILES])
+
+        for k in range(B * BLOCKS):
+            if k + 2 < B * BLOCKS:
+                load(k + 2)
+            if k + 1 < B * BLOCKS:
+                quantise(k + 1)
+            multiply_and_pool(k)

@@ -22,17 +22,14 @@ assert C == P * PACK and H == W
 
 WINDOW = 256
 BAND = WINDOW // W
-BLOCK_ROWS = 32
-BLOCKS = H // BLOCK_ROWS
-BLOCK_PIXELS = BLOCK_ROWS * W
-BANDS = BLOCK_ROWS // BAND
-STRIP = WINDOW // BLOCK_ROWS
-STRIPS = W // STRIP
-
 CHUNK_ROWS = 8
-CHUNKS = BLOCK_ROWS // CHUNK_ROWS
 CHUNK_PIXELS = CHUNK_ROWS * W
-VECTOR_CHUNK = 1
+FIRST_IMAGE_BLOCKS = (16, 16, 32)
+IMAGE_BLOCKS = (32, 32)
+FIRST_PIECES = ((0, 4), (4, 4), (8, 8))
+LOADS_AHEAD = 6
+FINISH_DELAY = 2
+IDENTITY = mybir.ActivationFunctionType.Identity
 
 W_PAD = 48
 W_SLOT = 256
@@ -45,52 +42,79 @@ def tile_pam_module_pa_t_kernel(tc, x, Wq, bq, Wk, bk, Wv, bv, out_0, out_1, out
     with ExitStack() as ctx:
         const = ctx.enter_context(tc.tile_pool(name="const", bufs=1))
         keep = ctx.enter_context(tc.tile_pool(name="keep", bufs=B))
-        raw_pool = ctx.enter_context(tc.tile_pool(name="raw", bufs=2 * CHUNKS))
-        grouped_pool = ctx.enter_context(tc.tile_pool(name="grouped", bufs=CHUNKS))
-        small = ctx.enter_context(tc.tile_pool(name="small", bufs=2))
+        raw_pool = ctx.enter_context(tc.tile_pool(name="raw", bufs=8))
+        grouped_pool = ctx.enter_context(tc.tile_pool(name="grouped", bufs=4))
+        small = ctx.enter_context(tc.tile_pool(name="small", bufs=4))
         column_psum = ctx.enter_context(tc.psum_pool(name="column_psum", bufs=O_TILES))
         psum = ctx.enter_context(tc.psum_pool(name="psum", bufs=8 - O_TILES))
         ctx.enter_context(tc.manual_schedule())
 
+        blocks = []
+        for n in range(B):
+            first_row = 0
+            for rows in FIRST_IMAGE_BLOCKS if n == 0 else IMAGE_BLOCKS:
+                blocks.append((n, first_row, rows))
+                first_row += rows
+        K = len(blocks)
+
+        def pieces(k):
+            if k == 0:
+                return FIRST_PIECES
+            return tuple((offset, CHUNK_ROWS) for offset in range(0, blocks[k][2], CHUNK_ROWS))
+
         x_channels = x.rearrange("n (p t) h w -> n p t (h w)", t=PACK)
-        raw_chunks = {}
+        raw_pieces = {}
+        grouped_pieces = {}
         quantised = {}
         pooling = {}
+        row_accs = {}
 
-        def load(k):
-            n, block = divmod(k, BLOCKS)
-            raw_chunks[k] = []
-            for c in range(CHUNKS):
-                first = block * BLOCK_PIXELS + c * CHUNK_PIXELS
-                raw = raw_pool.tile([P, PACK, CHUNK_PIXELS], BF16, name="raw")
-                nc.sync.dma_start(out=raw[:], in_=x_channels[n, :, :, first : first + CHUNK_PIXELS])
-                raw_chunks[k].append(raw)
+        def load_piece(k, index):
+            n, first_row, rows = blocks[k]
+            offset, piece_rows = pieces(k)[index]
+            first = (first_row + offset) * W
+            pixels = piece_rows * W
+            raw = raw_pool.tile([P, PACK, CHUNK_PIXELS], BF16, name="raw")
+            nc.sync.dma_start(out=raw[:, :, 0:pixels], in_=x_channels[n, :, :, first : first + pixels])
+            raw_pieces[(k, index)] = raw
 
-        def quantise(k):
-            n, block = divmod(k, BLOCKS)
+        def regroup(k, index):
+            offset, piece_rows = pieces(k)[index]
+            pixels = piece_rows * W
+            grouped = grouped_pool.tile([P, CHUNK_PIXELS * PACK], BF16, align_bytes=64, name="grouped")
+            grouped_view = grouped[:, 0 : pixels * PACK].rearrange("p (q i t) -> p q t i", i=4, t=PACK)
+            raw_view = raw_pieces[(k, index)][:, :, 0:pixels].rearrange("p t (q i) -> p q t i", i=4)
+            if offset == CHUNK_ROWS:
+                nc.vector.tensor_copy(out=grouped_view, in_=raw_view)
+            else:
+                nc.scalar.copy(out=grouped_view, in_=raw_view)
+            grouped_pieces[(k, index)] = grouped
+
+        def quantise(k, index):
+            n, first_row, rows = blocks[k]
+            offset, piece_rows = pieces(k)[index]
+            first = (first_row + offset) * W
+            pixels = piece_rows * W
+            codes_by_row, scales_by_row = quantised[n][0:2]
+            nc.vector.quantize_mx(
+                out=codes_by_row[:, first : first + pixels].bitcast(FP8X4),
+                scales=scales_by_row[:, first : first + pixels],
+                in_=grouped_pieces[(k, index)][:, 0 : pixels * PACK],
+            )
+
+        def to_strips(k, from_row, to_row):
+            n, first_row, rows = blocks[k]
             codes_by_row, scales_by_row, codes_by_strip, scales_by_strip = quantised[n]
-            for c in range(CHUNKS):
-                first = block * BLOCK_PIXELS + c * CHUNK_PIXELS
-                grouped = grouped_pool.tile([P, CHUNK_PIXELS * PACK], BF16, align_bytes=64)
-                grouped_view = grouped[:].rearrange("p (q i t) -> p q t i", i=4, t=PACK)
-                raw_view = raw_chunks[k][c][:].rearrange("p t (q i) -> p q t i", i=4)
-                if c == VECTOR_CHUNK:
-                    nc.vector.tensor_copy(out=grouped_view, in_=raw_view)
-                else:
-                    nc.scalar.copy(out=grouped_view, in_=raw_view)
-                nc.vector.quantize_mx(
-                    out=codes_by_row[:, first : first + CHUNK_PIXELS].bitcast(FP8X4),
-                    scales=scales_by_row[:, first : first + CHUNK_PIXELS],
-                    in_=grouped[:],
-                )
-            pixels = slice(block * BLOCK_PIXELS, (block + 1) * BLOCK_PIXELS)
+            strip = WINDOW // rows
+            strips = W // strip
+            pixels = slice(first_row * W, (first_row + rows) * W)
             nc.vector.tensor_copy(
-                out=codes_by_strip[:, pixels].bitcast(I32).rearrange("p (s i j) -> p s i j", s=STRIPS, j=STRIP),
-                in_=codes_by_row[:, pixels].bitcast(I32).rearrange("p (i s j) -> p s i j", s=STRIPS, j=STRIP),
+                out=codes_by_strip[:, pixels].bitcast(I32).rearrange("p (s i j) -> p s i j", s=strips, j=strip)[:, :, from_row:to_row, :],
+                in_=codes_by_row[:, pixels].bitcast(I32).rearrange("p (i s j) -> p s i j", s=strips, j=strip)[:, :, from_row:to_row, :],
             )
             nc.vector.tensor_copy(
-                out=scales_by_strip[:, pixels].bitcast(I32).rearrange("p (s i j) -> p s i j", s=STRIPS, j=STRIP // 4),
-                in_=scales_by_row[:, pixels].bitcast(I32).rearrange("p (i s j) -> p s i j", s=STRIPS, j=STRIP // 4),
+                out=scales_by_strip[:, pixels].bitcast(I32).rearrange("p (s i j) -> p s i j", s=strips, j=strip // 4)[:, :, from_row:to_row, :],
+                in_=scales_by_row[:, pixels].bitcast(I32).rearrange("p (i s j) -> p s i j", s=strips, j=strip // 4)[:, :, from_row:to_row, :],
             )
 
         def product(acc, r, codes, scales, window, first, last):
@@ -105,52 +129,60 @@ def tile_pam_module_pa_t_kernel(tc, x, Wq, bq, Wk, bk, Wv, bv, out_0, out_1, out
                 stop=last,
             )
 
-        def multiply_and_pool(k):
-            n, block = divmod(k, BLOCKS)
-            codes_by_row, scales_by_row, codes_by_strip, scales_by_strip = quantised[n]
-            if block == 0:
-                sums = small.tile([P, O_TILES, H + W], F32)
+        def column_passes(k, index):
+            n, first_row, rows = blocks[k]
+            offset, piece_rows = pieces(k)[index]
+            codes_by_row, scales_by_row = quantised[n][0:2]
+            if first_row + offset == 0:
+                sums = small.tile([P, O_TILES, H + W], F32, name="sums")
                 column_acc = [column_psum.tile([P, WINDOW], F32, name="column_acc", tag="bank") for r in range(O_TILES)]
                 pooling[n] = (sums, column_acc)
             sums, column_acc = pooling[n]
-            last_block = block == BLOCKS - 1
-            for band in range(BANDS):
+            for window in range((first_row + offset) // BAND, (first_row + offset + piece_rows) // BAND):
                 for r in range(O_TILES):
-                    product(column_acc[r], r, codes_by_row, scales_by_row, block * BANDS + band,
-                            block == 0 and band == 0, last_block and band == BANDS - 1)
-            if last_block:
-                for r in range(O_TILES):
-                    nc.vector.tensor_reduce(
-                        out=sums[:, r, H : H + W],
-                        in_=column_acc[r][:].rearrange("p (i j) -> p j i", i=BAND),
-                        axis=X_AXIS,
-                        op=ADD,
-                    )
-            pooled_to = [out_0[n], out_1[n], out_2[n, 0:P], out_2[n, P : 2 * P]]
+                    product(column_acc[r], r, codes_by_row, scales_by_row, window, window == 0, window == H // BAND - 1)
+
+        def column_sums(n):
+            sums, column_acc = pooling[n]
             for r in range(O_TILES):
-                row_acc = psum.tile([P, WINDOW], F32, tag="bank")
-                for strip in range(STRIPS):
-                    product(row_acc, r, codes_by_strip, scales_by_strip, block * STRIPS + strip,
-                            strip == 0, strip == STRIPS - 1)
                 nc.vector.tensor_reduce(
-                    out=sums[:, r, block * BLOCK_ROWS : (block + 1) * BLOCK_ROWS],
-                    in_=row_acc[:].rearrange("p (i j) -> p i j", j=STRIP),
+                    out=sums[:, r, H : H + W],
+                    in_=column_acc[r][:].rearrange("p (i j) -> p j i", i=BAND),
                     axis=X_AXIS,
                     op=ADD,
                 )
-                if last_block:
-                    pooled = small.tile([P, H + W], F32)
-                    nc.vector.tensor_scalar(
-                        out=pooled[:], in0=sums[:, r, :], scalar1=1.0 / W, scalar2=bias[:, r : r + 1],
-                        op0=MULT, op1=ADD,
-                    )
-                    nc.sync.dma_start(out=pooled_to[r], in_=pooled[:])
+
+        def row_passes(k):
+            n, first_row, rows = blocks[k]
+            codes_by_strip, scales_by_strip = quantised[n][2:4]
+            strips = rows // BAND
+            row_accs[k] = []
+            for r in range(O_TILES):
+                row_acc = psum.tile([P, WINDOW], F32, name="row_acc", tag="bank")
+                for s in range(strips):
+                    product(row_acc, r, codes_by_strip, scales_by_strip, first_row // BAND + s, s == 0, s == strips - 1)
+                row_accs[k].append(row_acc)
+
+        def row_sums(k, r):
+            n, first_row, rows = blocks[k]
+            nc.vector.tensor_reduce(
+                out=pooling[n][0][:, r, first_row : first_row + rows],
+                in_=row_accs[k][r][:].rearrange("p (i j) -> p i j", j=WINDOW // rows),
+                axis=X_AXIS,
+                op=ADD,
+            )
+
+        def finish(n, r):
+            pooled_to = [out_0[n], out_1[n], out_2[n, 0:P], out_2[n, P : 2 * P]]
+            pooled = small.tile([P, H + W], F32, name="pooled")
+            nc.scalar.activation(out=pooled[:], in_=pooling[n][0][:, r, :], func=IDENTITY, bias=bias[:, r : r + 1], scale=1.0 / W)
+            nc.sync.dma_start(out=pooled_to[r], in_=pooled[:])
 
         for n in range(B):
-            codes_by_row = keep.tile([P, PIXELS], U32, align_bytes=256)
-            scales_by_row = keep.tile([P, PIXELS], U8, align_bytes=256)
-            codes_by_strip = keep.tile([P, PIXELS], U32, align_bytes=256)
-            scales_by_strip = keep.tile([P, PIXELS], U8, align_bytes=256)
+            codes_by_row = keep.tile([P, PIXELS], U32, align_bytes=256, name="codes_by_row")
+            scales_by_row = keep.tile([P, PIXELS], U8, align_bytes=256, name="scales_by_row")
+            codes_by_strip = keep.tile([P, PIXELS], U32, align_bytes=256, name="codes_by_strip")
+            scales_by_strip = keep.tile([P, PIXELS], U8, align_bytes=256, name="scales_by_strip")
             nc.vector.memset(scales_by_row[:].bitcast(I32), 0)
             quantised[n] = (codes_by_row, scales_by_row, codes_by_strip, scales_by_strip)
 
@@ -167,44 +199,86 @@ def tile_pam_module_pa_t_kernel(tc, x, Wq, bq, Wk, bk, Wv, bv, out_0, out_1, out
         w_rows = const.tile([P, O_TILES * C], BF16)
         nc.sync.dma_start(out=w_rows[:, 0:C], in_=Wq)
         nc.sync.dma_start(out=w_rows[:, C : 2 * C], in_=Wk)
+        sequence = [(k, index) for k in range(K) for index in range(len(pieces(k)))]
+        load_piece(*sequence[0])
         nc.sync.dma_start(
             out=w_rows[:, 2 * C : 4 * C].rearrange("o (r c) -> o r c", r=2),
             in_=Wv.rearrange("(r o) c -> o r c", r=2),
         )
-        load(0)
-        load(1)
+        for step in range(1, LOADS_AHEAD):
+            load_piece(*sequence[step])
 
         w_pairs = w_rows[:].bitcast(F32).rearrange("o (r p u) -> o r u p", r=O_TILES, u=2)
         w_grouped = const.tile([P, O_TILES * P * PACK], BF16, align_bytes=64)
         w_grouped_pairs = w_grouped[:].bitcast(F32).rearrange("p (r o u) -> p r o u", r=O_TILES, u=2)
+        w_codes = const.tile([P, W_PAD + O_TILES * P], U32, align_bytes=256)
+        w_scales = const.tile([P, O_TILES * W_SLOT], U8, align_bytes=256)
+        turned_halves = []
         for half in range(2):
-            turned = psum.tile([P, 2, 2, P], F32, tag="bank")
+            turned = psum.tile([P, 2, 2, P], F32, name="turned", tag="bank")
             for r in range(2):
                 for u in range(2):
                     nc.tensor.transpose(turned[:, r, u, :], w_pairs[:, 2 * half + r, u, :], identity[:])
+            turned_halves.append(turned)
+
+        def weights_out(half):
             nc.vector.tensor_copy(
                 out=w_grouped_pairs[:, 2 * half : 2 * half + 2],
-                in_=turned[:].rearrange("p r u o -> p r o u"),
+                in_=turned_halves[half][:].rearrange("p r u o -> p r o u"),
             )
-        w_codes = const.tile([P, W_PAD + O_TILES * P], U32, align_bytes=256)
-        w_scales = const.tile([P, O_TILES * W_SLOT], U8, align_bytes=256)
+
+        def weights_quantise(half):
+            for r in range(2 * half, 2 * half + 2):
+                nc.vector.quantize_mx(
+                    out=w_codes[:, W_PAD + r * P : W_PAD + (r + 1) * P].bitcast(FP8X4),
+                    scales=w_scales[:, r * W_SLOT : r * W_SLOT + P],
+                    in_=w_grouped[:, r * P * PACK : (r + 1) * P * PACK],
+                )
+
+        weights_out(0)
+        regroup(*sequence[0])
+        regroup(*sequence[1])
+        weights_quantise(0)
+        quantise(*sequence[0])
+        weights_out(1)
+        weights_quantise(1)
+
+        rows_in_psum = []
+        to_finish = []
+        for step in range(len(sequence)):
+            k, index = sequence[step]
+            n, first_row, rows = blocks[k]
+            last_piece = index == len(pieces(k)) - 1
+            if step + LOADS_AHEAD < len(sequence):
+                load_piece(*sequence[step + LOADS_AHEAD])
+            if step + 2 < len(sequence):
+                regroup(*sequence[step + 2])
+            if step + 1 < len(sequence):
+                quantise(*sequence[step + 1])
+            if last_piece:
+                to_strips(k, 0, rows)
+                for earlier in rows_in_psum:
+                    for r in range(O_TILES):
+                        row_sums(earlier, r)
+                    if blocks[earlier][1] + blocks[earlier][2] == H:
+                        to_finish.append((step + FINISH_DELAY, blocks[earlier][0]))
+                rows_in_psum.clear()
+            column_passes(k, index)
+            if last_piece:
+                if first_row + rows == H:
+                    column_sums(n)
+                if k == 1:
+                    bias_turned = psum.tile([P, P], F32, name="bias_turned", tag="bank")
+                    nc.tensor.transpose(bias_turned[:], bias_rows_f32[:], identity[:])
+                    bias = const.tile([P, O_TILES], F32)
+                    nc.vector.tensor_copy(out=bias[:], in_=bias_turned[:, 0:O_TILES])
+                row_passes(k)
+                rows_in_psum.append(k)
+            for due, image in list(to_finish):
+                if step >= due:
+                    for r in range(O_TILES):
+                        finish(image, r)
+                    to_finish.remove((due, image))
         for r in range(O_TILES):
-            nc.vector.quantize_mx(
-                out=w_codes[:, W_PAD + r * P : W_PAD + (r + 1) * P].bitcast(FP8X4),
-                scales=w_scales[:, r * W_SLOT : r * W_SLOT + P],
-                in_=w_grouped[:, r * P * PACK : (r + 1) * P * PACK],
-            )
-
-        quantise(0)
-
-        bias_turned = psum.tile([P, P], F32, tag="bank")
-        nc.tensor.transpose(bias_turned[:], bias_rows_f32[:], identity[:])
-        bias = const.tile([P, O_TILES], F32)
-        nc.vector.tensor_copy(out=bias[:], in_=bias_turned[:, 0:O_TILES])
-
-        for k in range(B * BLOCKS):
-            if k + 2 < B * BLOCKS:
-                load(k + 2)
-            if k + 1 < B * BLOCKS:
-                quantise(k + 1)
-            multiply_and_pool(k)
+            row_sums(K - 1, r)
+            finish(B - 1, r)

@@ -25,7 +25,9 @@ BAND = WINDOW // W
 CHUNK_ROWS = 8
 CHUNK_PIXELS = CHUNK_ROWS * W
 FIRST_IMAGE_BLOCKS = (16, 16, 32)
-IMAGE_BLOCKS = (32, 32)
+IMAGE_BLOCKS = (64,)
+STRIP_PIECES = 4
+WIDE = 512
 FIRST_PIECES = ((0, 4), (4, 4), (8, 8))
 LOADS_AHEAD = 6
 FINISH_DELAY = 2
@@ -84,7 +86,7 @@ def tile_pam_module_pa_t_kernel(tc, x, Wq, bq, Wk, bk, Wv, bv, out_0, out_1, out
             grouped = grouped_pool.tile([P, CHUNK_PIXELS * PACK], BF16, align_bytes=64, name="grouped")
             grouped_view = grouped[:, 0 : pixels * PACK].rearrange("p (q i t) -> p q t i", i=4, t=PACK)
             raw_view = raw_pieces[(k, index)][:, :, 0:pixels].rearrange("p t (q i) -> p q t i", i=4)
-            if offset == CHUNK_ROWS:
+            if offset % (4 * CHUNK_ROWS) == CHUNK_ROWS:
                 nc.vector.tensor_copy(out=grouped_view, in_=raw_view)
             else:
                 nc.scalar.copy(out=grouped_view, in_=raw_view)
@@ -105,7 +107,7 @@ def tile_pam_module_pa_t_kernel(tc, x, Wq, bq, Wk, bk, Wv, bv, out_0, out_1, out
         def to_strips(k, from_row, to_row):
             n, first_row, rows = blocks[k]
             codes_by_row, scales_by_row, codes_by_strip, scales_by_strip = quantised[n]
-            strip = WINDOW // rows
+            strip = row_window(k) // rows
             strips = W // strip
             pixels = slice(first_row * W, (first_row + rows) * W)
             nc.vector.tensor_copy(
@@ -117,8 +119,11 @@ def tile_pam_module_pa_t_kernel(tc, x, Wq, bq, Wk, bk, Wv, bv, out_0, out_1, out
                 in_=scales_by_row[:, pixels].bitcast(I32).rearrange("p (i s j) -> p s i j", s=strips, j=strip // 4)[:, :, from_row:to_row, :],
             )
 
-        def product(acc, r, codes, scales, window, first, last):
-            pixels = slice(window * WINDOW, (window + 1) * WINDOW)
+        def row_window(k):
+            return WIDE if blocks[k][2] == H else WINDOW
+
+        def product(acc, r, codes, scales, first_pixel, width, first, last):
+            pixels = slice(first_pixel, first_pixel + width)
             nc.tensor.matmul_mx(
                 out=acc[:],
                 lhsT=w_codes[:, W_PAD + r * P : W_PAD + (r + 1) * P].bitcast(FP8X4),
@@ -140,7 +145,7 @@ def tile_pam_module_pa_t_kernel(tc, x, Wq, bq, Wk, bk, Wv, bv, out_0, out_1, out
             sums, column_acc = pooling[n]
             for window in range((first_row + offset) // BAND, (first_row + offset + piece_rows) // BAND):
                 for r in range(O_TILES):
-                    product(column_acc[r], r, codes_by_row, scales_by_row, window, window == 0, window == H // BAND - 1)
+                    product(column_acc[r], r, codes_by_row, scales_by_row, window * WINDOW, WINDOW, window == 0, window == H // BAND - 1)
 
         def column_sums(n):
             sums, column_acc = pooling[n]
@@ -155,19 +160,20 @@ def tile_pam_module_pa_t_kernel(tc, x, Wq, bq, Wk, bk, Wv, bv, out_0, out_1, out
         def row_passes(k):
             n, first_row, rows = blocks[k]
             codes_by_strip, scales_by_strip = quantised[n][2:4]
-            strips = rows // BAND
+            width = row_window(k)
+            strips = rows * W // width
             row_accs[k] = []
             for r in range(O_TILES):
-                row_acc = psum.tile([P, WINDOW], F32, name="row_acc", tag="bank")
+                row_acc = psum.tile([P, width], F32, name="row_acc", tag="bank")
                 for s in range(strips):
-                    product(row_acc, r, codes_by_strip, scales_by_strip, first_row // BAND + s, s == 0, s == strips - 1)
+                    product(row_acc, r, codes_by_strip, scales_by_strip, first_row * W + s * width, width, s == 0, s == strips - 1)
                 row_accs[k].append(row_acc)
 
         def row_sums(k, r):
             n, first_row, rows = blocks[k]
             nc.vector.tensor_reduce(
                 out=pooling[n][0][:, r, first_row : first_row + rows],
-                in_=row_accs[k][r][:].rearrange("p (i j) -> p i j", j=WINDOW // rows),
+                in_=row_accs[k][r][:].rearrange("p (i j) -> p i j", j=row_window(k) // rows),
                 axis=X_AXIS,
                 op=ADD,
             )
@@ -243,6 +249,7 @@ def tile_pam_module_pa_t_kernel(tc, x, Wq, bq, Wk, bk, Wv, bv, out_0, out_1, out
         weights_out(1)
         weights_quantise(1)
 
+        strips_done = 0
         rows_in_psum = []
         to_finish = []
         for step in range(len(sequence)):
@@ -255,8 +262,11 @@ def tile_pam_module_pa_t_kernel(tc, x, Wq, bq, Wk, bk, Wv, bv, out_0, out_1, out
                 regroup(*sequence[step + 2])
             if step + 1 < len(sequence):
                 quantise(*sequence[step + 1])
+            if last_piece or (index + 1) % STRIP_PIECES == 0:
+                piece_end = pieces(k)[index][0] + pieces(k)[index][1]
+                to_strips(k, strips_done, piece_end)
+                strips_done = 0 if last_piece else piece_end
             if last_piece:
-                to_strips(k, 0, rows)
                 for earlier in rows_in_psum:
                     for r in range(O_TILES):
                         row_sums(earlier, r)
@@ -279,6 +289,9 @@ def tile_pam_module_pa_t_kernel(tc, x, Wq, bq, Wk, bk, Wv, bv, out_0, out_1, out
                     for r in range(O_TILES):
                         finish(image, r)
                     to_finish.remove((due, image))
+        for due, image in to_finish:
+            for r in range(O_TILES):
+                finish(image, r)
         for r in range(O_TILES):
             row_sums(K - 1, r)
             finish(B - 1, r)

@@ -24,8 +24,7 @@ WINDOW = 256
 BAND = WINDOW // W
 CHUNK_ROWS = 8
 CHUNK_PIXELS = CHUNK_ROWS * W
-FIRST_IMAGE_BLOCKS = (16, 16, 32)
-IMAGE_BLOCKS = (64,)
+IMAGE_BLOCKS = ((16, 16, 32), (32, 32), (64,), (64,))
 STRIP_PIECES = 4
 WIDE = 512
 FIRST_PIECES = ((0, 4), (4, 4), (8, 8))
@@ -54,7 +53,7 @@ def tile_pam_module_pa_t_kernel(tc, x, Wq, bq, Wk, bk, Wv, bv, out_0, out_1, out
         blocks = []
         for n in range(B):
             first_row = 0
-            for rows in FIRST_IMAGE_BLOCKS if n == 0 else IMAGE_BLOCKS:
+            for rows in IMAGE_BLOCKS[n]:
                 blocks.append((n, first_row, rows))
                 first_row += rows
         K = len(blocks)
@@ -82,11 +81,12 @@ def tile_pam_module_pa_t_kernel(tc, x, Wq, bq, Wk, bk, Wv, bv, out_0, out_1, out
 
         def regroup(k, index):
             offset, piece_rows = pieces(k)[index]
+            row = blocks[k][1] + offset
             pixels = piece_rows * W
             grouped = grouped_pool.tile([P, CHUNK_PIXELS * PACK], BF16, align_bytes=64, name="grouped")
             grouped_view = grouped[:, 0 : pixels * PACK].rearrange("p (q i t) -> p q t i", i=4, t=PACK)
             raw_view = raw_pieces[(k, index)][:, :, 0:pixels].rearrange("p t (q i) -> p q t i", i=4)
-            if offset % (4 * CHUNK_ROWS) == CHUNK_ROWS:
+            if row % 32 == 16 or (blocks[k][0] == 0 and row == 32):
                 nc.vector.tensor_copy(out=grouped_view, in_=raw_view)
             else:
                 nc.scalar.copy(out=grouped_view, in_=raw_view)

@@ -28,6 +28,7 @@ IMAGE_BLOCKS = ((16, 16, 32), (32, 32), (64,), (64,))
 STRIP_PIECES = 4
 WIDE = 512
 FIRST_PIECES = ((0, 4), (4, 4), (8, 8))
+RUN = 8
 LOADS_AHEAD = 6
 FINISH_DELAY = 2
 IDENTITY = mybir.ActivationFunctionType.Identity
@@ -84,8 +85,8 @@ def tile_pam_module_pa_t_kernel(tc, x, Wq, bq, Wk, bk, Wv, bv, out_0, out_1, out
             row = blocks[k][1] + offset
             pixels = piece_rows * W
             grouped = grouped_pool.tile([P, CHUNK_PIXELS * PACK], BF16, align_bytes=64, name="grouped")
-            grouped_view = grouped[:, 0 : pixels * PACK].rearrange("p (q i t) -> p q t i", i=4, t=PACK)
-            raw_view = raw_pieces[(k, index)][:, :, 0:pixels].rearrange("p t (q i) -> p q t i", i=4)
+            grouped_view = grouped[:, 0 : pixels * PACK].rearrange("p (q i t) -> p q t i", i=RUN, t=PACK)
+            raw_view = raw_pieces[(k, index)][:, :, 0:pixels].rearrange("p t (q i) -> p q t i", i=RUN)
             if row % 32 == 16 or (blocks[k][0] == 0 and row == 32):
                 nc.vector.tensor_copy(out=grouped_view, in_=raw_view)
             else:

@@ -27,9 +27,9 @@ CHUNK_PIXELS = CHUNK_ROWS * W
 IMAGE_BLOCKS = ((16, 16, 32), (32, 32), (64,), (64,))
 STRIP_PIECES = 4
 WIDE = 512
-FIRST_PIECES = ((0, 4), (4, 4), (8, 8))
+FIRST_PIECES = ((0, 4), (4, 4), (8, 4), (12, 4))
 RUN = 8
-LOADS_AHEAD = 6
+LOADS_AHEAD = 7
 FINISH_DELAY = 2
 IDENTITY = mybir.ActivationFunctionType.Identity
 
@@ -87,7 +87,7 @@ def tile_pam_module_pa_t_kernel(tc, x, Wq, bq, Wk, bk, Wv, bv, out_0, out_1, out
             grouped = grouped_pool.tile([P, CHUNK_PIXELS * PACK], BF16, align_bytes=64, name="grouped")
             grouped_view = grouped[:, 0 : pixels * PACK].rearrange("p (q i t) -> p q t i", i=RUN, t=PACK)
             raw_view = raw_pieces[(k, index)][:, :, 0:pixels].rearrange("p t (q i) -> p q t i", i=RUN)
-            if row % 32 == 16 or (blocks[k][0] == 0 and row == 32):
+            if (row == 12 or (row % 16 == 8 and row > 8)) if blocks[k][0] == 0 else row % 32 == 16:
                 nc.vector.tensor_copy(out=grouped_view, in_=raw_view)
             else:
                 nc.scalar.copy(out=grouped_view, in_=raw_view)
@@ -190,8 +190,13 @@ def tile_pam_module_pa_t_kernel(tc, x, Wq, bq, Wk, bk, Wv, bv, out_0, out_1, out
             scales_by_row = keep.tile([P, PIXELS], U8, align_bytes=256, name="scales_by_row")
             codes_by_strip = keep.tile([P, PIXELS], U32, align_bytes=256, name="codes_by_strip")
             scales_by_strip = keep.tile([P, PIXELS], U8, align_bytes=256, name="scales_by_strip")
-            nc.vector.memset(scales_by_row[:].bitcast(I32), 0)
             quantised[n] = (codes_by_row, scales_by_row, codes_by_strip, scales_by_strip)
+
+        def clear_scales(n):
+            nc.vector.memset(quantised[n][1][:].bitcast(I32), 0)
+
+        clear_scales(0)
+        clear_scales(1)
 
         bias_rows = const.tile([P, P], BF16)
         nc.gpsimd.memset(bias_rows[:], 0.0)
@@ -259,14 +264,16 @@ def tile_pam_module_pa_t_kernel(tc, x, Wq, bq, Wk, bk, Wv, bv, out_0, out_1, out
             last_piece = index == len(pieces(k)) - 1
             if step + LOADS_AHEAD < len(sequence):
                 load_piece(*sequence[step + LOADS_AHEAD])
-            if step + 2 < len(sequence):
-                regroup(*sequence[step + 2])
-            if step + 1 < len(sequence):
-                quantise(*sequence[step + 1])
+            piece_end = pieces(k)[index][0] + pieces(k)[index][1]
             if last_piece or (index + 1) % STRIP_PIECES == 0:
-                piece_end = pieces(k)[index][0] + pieces(k)[index][1]
                 to_strips(k, strips_done, piece_end)
                 strips_done = 0 if last_piece else piece_end
+            if step + 2 < len(sequence):
+                regroup(*sequence[step + 2])
+            if 1 <= n < B - 1 and first_row + pieces(k)[index][0] == H // 2:
+                clear_scales(n + 1)
+            if step + 1 < len(sequence):
+                quantise(*sequence[step + 1])
             if last_piece:
                 for earlier in rows_in_psum:
                     for r in range(O_TILES):
@@ -278,7 +285,7 @@ def tile_pam_module_pa_t_kernel(tc, x, Wq, bq, Wk, bk, Wv, bv, out_0, out_1, out
             if last_piece:
                 if first_row + rows == H:
                     column_sums(n)
-                if k == 1:
+                if k == 0:
                     bias_turned = psum.tile([P, P], F32, name="bias_turned", tag="bank")
                     nc.tensor.transpose(bias_turned[:], bias_rows_f32[:], identity[:])
                     bias = const.tile([P, O_TILES], F32)

@@ -58,6 +58,10 @@ def tile_pam_module_pa_t_kernel(tc, x, Wq, bq, Wk, bk, Wv, bv, out_0, out_1, out
                 blocks.append((n, first_row, rows))
                 first_row += rows
         K = len(blocks)
+        second_of = {}
+        for k in range(1, K):
+            if blocks[k][0] == blocks[k - 1][0] and blocks[k][2] == blocks[k - 1][2] and k - 1 not in second_of:
+                second_of[k] = k - 1
 
         def pieces(k):
             if k == 0:
@@ -126,7 +130,7 @@ def tile_pam_module_pa_t_kernel(tc, x, Wq, bq, Wk, bk, Wv, bv, out_0, out_1, out
         def product(acc, r, codes, scales, first_pixel, width, first, last):
             pixels = slice(first_pixel, first_pixel + width)
             nc.tensor.matmul_mx(
-                out=acc[:],
+                out=acc,
                 lhsT=w_codes[:, W_PAD + r * P : W_PAD + (r + 1) * P].bitcast(FP8X4),
                 lhsT_scale=w_scales[:, r * W_SLOT : r * W_SLOT + P],
                 rhs=codes[:, pixels].bitcast(FP8X4),
@@ -146,7 +150,7 @@ def tile_pam_module_pa_t_kernel(tc, x, Wq, bq, Wk, bk, Wv, bv, out_0, out_1, out
             sums, column_acc = pooling[n]
             for window in range((first_row + offset) // BAND, (first_row + offset + piece_rows) // BAND):
                 for r in range(O_TILES):
-                    product(column_acc[r], r, codes_by_row, scales_by_row, window * WINDOW, WINDOW, window == 0, window == H // BAND - 1)
+                    product(column_acc[r][:], r, codes_by_row, scales_by_row, window * WINDOW, WINDOW, window == 0, window == H // BAND - 1)
 
         def column_sums(n):
             sums, column_acc = pooling[n]
@@ -163,18 +167,24 @@ def tile_pam_module_pa_t_kernel(tc, x, Wq, bq, Wk, bk, Wv, bv, out_0, out_1, out
             codes_by_strip, scales_by_strip = quantised[n][2:4]
             width = row_window(k)
             strips = rows * W // width
-            row_accs[k] = []
+            if k in second_of:
+                row_accs[k] = row_accs[second_of[k]]
+            else:
+                row_accs[k] = [psum.tile([P, WIDE], F32, name="row_acc", tag="bank") for r in range(O_TILES)]
+            first_column = WINDOW if k in second_of else 0
             for r in range(O_TILES):
-                row_acc = psum.tile([P, width], F32, name="row_acc", tag="bank")
                 for s in range(strips):
-                    product(row_acc, r, codes_by_strip, scales_by_strip, first_row * W + s * width, width, s == 0, s == strips - 1)
-                row_accs[k].append(row_acc)
+                    product(row_accs[k][r][:, first_column : first_column + width], r, codes_by_strip, scales_by_strip,
+                            first_row * W + s * width, width, s == 0, s == strips - 1)
 
         def row_sums(k, r):
             n, first_row, rows = blocks[k]
+            strip = row_window(k) // rows
+            if k + 1 in second_of:
+                rows = 2 * rows
             nc.vector.tensor_reduce(
                 out=pooling[n][0][:, r, first_row : first_row + rows],
-                in_=row_accs[k][r][:].rearrange("p (i j) -> p i j", j=row_window(k) // rows),
+                in_=row_accs[k][r][:, 0 : rows * strip].rearrange("p (i j) -> p i j", j=strip),
                 axis=X_AXIS,
                 op=ADD,
             )
@@ -274,11 +284,11 @@ def tile_pam_module_pa_t_kernel(tc, x, Wq, bq, Wk, bk, Wv, bv, out_0, out_1, out
                 clear_scales(n + 1)
             if step + 1 < len(sequence):
                 quantise(*sequence[step + 1])
-            if last_piece:
+            if last_piece and k not in second_of:
                 for earlier in rows_in_psum:
                     for r in range(O_TILES):
                         row_sums(earlier, r)
-                    if blocks[earlier][1] + blocks[earlier][2] == H:
+                    if blocks[earlier][1] + blocks[earlier][2] * (2 if earlier + 1 in second_of else 1) == H:
                         to_finish.append((step + FINISH_DELAY, blocks[earlier][0]))
                 rows_in_psum.clear()
             column_passes(k, index)
@@ -291,7 +301,8 @@ def tile_pam_module_pa_t_kernel(tc, x, Wq, bq, Wk, bk, Wv, bv, out_0, out_1, out
                     bias = const.tile([P, O_TILES], F32)
                     nc.vector.tensor_copy(out=bias[:], in_=bias_turned[:, 0:O_TILES])
                 row_passes(k)
-                rows_in_psum.append(k)
+                if k not in second_of:
+                    rows_in_psum.append(k)
             for due, image in list(to_finish):
                 if step >= due:
                     for r in range(O_TILES):

@@ -22,15 +22,23 @@ assert C == P * PACK and H == W
 
 WINDOW = 256
 BAND = WINDOW // W
-CHUNK_ROWS = 8
-CHUNK_PIXELS = CHUNK_ROWS * W
-IMAGE_BLOCKS = ((16, 16, 32), (32, 32), (64,), (64,))
-STRIP_PIECES = 4
-WIDE = 512
-FIRST_PIECES = ((0, 4), (4, 4), (8, 4), (12, 4))
+PIECE_ROWS = 8
+PIECE_PIXELS = PIECE_ROWS * W
+FIRST_PIECE_ROWS = 4
+BANDS = ((0, 0, 16, 2), (0, 32, 32, 2), (1, 0, 64, 2), (0, 16, 16, 1), (2, 0, 64, 2), (3, 0, 64, 2))
+SCALE_TILES = (0, 1, 2, 1)
+STRIP_ROWS = 32
 RUN = 8
+REGROUP_AHEAD = 2
 LOADS_AHEAD = 7
-FINISH_DELAY = 2
+VECTOR_ROWS = ((12, 24, 40, 56), (16, 48), (16, 48), (16, 48))
+PACE = 0.7
+PACE_HEAD = 2
+ONCE_FROM = 130
+ONCE_EVERY = 12.0
+READ_DELAY = 12.0
+FINISH_DELAY = 18.0
+ONCE_DELAY = 2.0
 IDENTITY = mybir.ActivationFunctionType.Identity
 
 W_PAD = 48
@@ -45,74 +53,74 @@ def tile_pam_module_pa_t_kernel(tc, x, Wq, bq, Wk, bk, Wv, bv, out_0, out_1, out
         const = ctx.enter_context(tc.tile_pool(name="const", bufs=1))
         keep = ctx.enter_context(tc.tile_pool(name="keep", bufs=B))
         raw_pool = ctx.enter_context(tc.tile_pool(name="raw", bufs=8))
-        grouped_pool = ctx.enter_context(tc.tile_pool(name="grouped", bufs=4))
-        small = ctx.enter_context(tc.tile_pool(name="small", bufs=4))
+        grouped_pool = ctx.enter_context(tc.tile_pool(name="grouped", bufs=REGROUP_AHEAD + 2))
+        small = ctx.enter_context(tc.tile_pool(name="small", bufs=8))
         column_psum = ctx.enter_context(tc.psum_pool(name="column_psum", bufs=O_TILES))
-        psum = ctx.enter_context(tc.psum_pool(name="psum", bufs=8 - O_TILES))
+        row_psum = ctx.enter_context(tc.psum_pool(name="row_psum", bufs=2))
+        once_psum = ctx.enter_context(tc.psum_pool(name="once_psum", bufs=2))
         ctx.enter_context(tc.manual_schedule())
 
+        pieces = []
         blocks = []
-        for n in range(B):
-            first_row = 0
-            for rows in IMAGE_BLOCKS[n]:
-                blocks.append((n, first_row, rows))
-                first_row += rows
+        for n, band_row, band_rows, times in BANDS:
+            if times == 2:
+                blocks.append((n, band_row, band_rows))
+            step = PIECE_ROWS if len(blocks) > 1 else FIRST_PIECE_ROWS
+            for row in range(band_row, band_row + band_rows, step):
+                pieces.append((n, row, step, len(blocks) - 1 if times == 2 else None))
         K = len(blocks)
-        second_of = {}
-        for k in range(1, K):
-            if blocks[k][0] == blocks[k - 1][0] and blocks[k][2] == blocks[k - 1][2] and k - 1 not in second_of:
-                second_of[k] = k - 1
-
-        def pieces(k):
-            if k == 0:
-                return FIRST_PIECES
-            return tuple((offset, CHUNK_ROWS) for offset in range(0, blocks[k][2], CHUNK_ROWS))
+        first_windows = {}
+        last_windows = {}
+        last_blocks = {}
+        for k in range(K):
+            n, first_row, rows = blocks[k]
+            first_windows.setdefault(n, first_row // BAND)
+            last_windows[n] = (first_row + rows) // BAND - 1
+            last_blocks[n] = k
 
         x_channels = x.rearrange("n (p t) h w -> n p t (h w)", t=PACK)
         raw_pieces = {}
         grouped_pieces = {}
         quantised = {}
-        pooling = {}
+        sums = {}
+        column_accs = {}
         row_accs = {}
 
-        def load_piece(k, index):
-            n, first_row, rows = blocks[k]
-            offset, piece_rows = pieces(k)[index]
-            first = (first_row + offset) * W
-            pixels = piece_rows * W
-            raw = raw_pool.tile([P, PACK, CHUNK_PIXELS], BF16, name="raw")
-            nc.sync.dma_start(out=raw[:, :, 0:pixels], in_=x_channels[n, :, :, first : first + pixels])
-            raw_pieces[(k, index)] = raw
+        def pixels_of(piece):
+            n, first_row, rows, k = pieces[piece]
+            return slice(first_row * W, (first_row + rows) * W)
 
-        def regroup(k, index):
-            offset, piece_rows = pieces(k)[index]
-            row = blocks[k][1] + offset
-            pixels = piece_rows * W
-            grouped = grouped_pool.tile([P, CHUNK_PIXELS * PACK], BF16, align_bytes=64, name="grouped")
+        def load(piece):
+            n, first_row, rows, k = pieces[piece]
+            raw = raw_pool.tile([P, PACK, PIECE_PIXELS], BF16, name="raw")
+            nc.sync.dma_start(out=raw[:, :, 0 : rows * W], in_=x_channels[n, :, :, pixels_of(piece)])
+            raw_pieces[piece] = raw
+
+        def regroup(piece):
+            n, row, rows, k = pieces[piece]
+            pixels = rows * W
+            grouped = grouped_pool.tile([P, PIECE_PIXELS * PACK], BF16, align_bytes=64, name="grouped")
             grouped_view = grouped[:, 0 : pixels * PACK].rearrange("p (q i t) -> p q t i", i=RUN, t=PACK)
-            raw_view = raw_pieces[(k, index)][:, :, 0:pixels].rearrange("p t (q i) -> p q t i", i=RUN)
-            if (row == 12 or (row % 16 == 8 and row > 8)) if blocks[k][0] == 0 else row % 32 == 16:
+            raw_view = raw_pieces[piece][:, :, 0:pixels].rearrange("p t (q i) -> p q t i", i=RUN)
+            if row in VECTOR_ROWS[n]:
                 nc.vector.tensor_copy(out=grouped_view, in_=raw_view)
             else:
                 nc.scalar.copy(out=grouped_view, in_=raw_view)
-            grouped_pieces[(k, index)] = grouped
+            grouped_pieces[piece] = grouped
 
-        def quantise(k, index):
-            n, first_row, rows = blocks[k]
-            offset, piece_rows = pieces(k)[index]
-            first = (first_row + offset) * W
-            pixels = piece_rows * W
+        def quantise(piece):
+            n, first_row, rows, k = pieces[piece]
             codes_by_row, scales_by_row = quantised[n][0:2]
             nc.vector.quantize_mx(
-                out=codes_by_row[:, first : first + pixels].bitcast(FP8X4),
-                scales=scales_by_row[:, first : first + pixels],
-                in_=grouped_pieces[(k, index)][:, 0 : pixels * PACK],
+                out=codes_by_row[:, pixels_of(piece)].bitcast(FP8X4),
+                scales=scales_by_row[:, pixels_of(piece)],
+                in_=grouped_pieces[piece][:, 0 : rows * W * PACK],
             )
 
         def to_strips(k, from_row, to_row):
             n, first_row, rows = blocks[k]
             codes_by_row, scales_by_row, codes_by_strip, scales_by_strip = quantised[n]
-            strip = row_window(k) // rows
+            strip = WINDOW // rows
             strips = W // strip
             pixels = slice(first_row * W, (first_row + rows) * W)
             nc.vector.tensor_copy(
@@ -123,9 +131,6 @@ def tile_pam_module_pa_t_kernel(tc, x, Wq, bq, Wk, bk, Wv, bv, out_0, out_1, out
                 out=scales_by_strip[:, pixels].bitcast(I32).rearrange("p (s i j) -> p s i j", s=strips, j=strip // 4)[:, :, from_row:to_row, :],
                 in_=scales_by_row[:, pixels].bitcast(I32).rearrange("p (i s j) -> p s i j", s=strips, j=strip // 4)[:, :, from_row:to_row, :],
             )
-
-        def row_window(k):
-            return WIDE if blocks[k][2] == H else WINDOW
 
         def product(acc, r, codes, scales, first_pixel, width, first, last):
             pixels = slice(first_pixel, first_pixel + width)
@@ -139,74 +144,111 @@ def tile_pam_module_pa_t_kernel(tc, x, Wq, bq, Wk, bk, Wv, bv, out_0, out_1, out
                 stop=last,
             )
 
-        def column_passes(k, index):
-            n, first_row, rows = blocks[k]
-            offset, piece_rows = pieces(k)[index]
+        def column_passes(n, window):
             codes_by_row, scales_by_row = quantised[n][0:2]
-            if first_row + offset == 0:
-                sums = small.tile([P, O_TILES, H + W], F32, name="sums")
-                column_acc = [column_psum.tile([P, WINDOW], F32, name="column_acc", tag="bank") for r in range(O_TILES)]
-                pooling[n] = (sums, column_acc)
-            sums, column_acc = pooling[n]
-            for window in range((first_row + offset) // BAND, (first_row + offset + piece_rows) // BAND):
+            first = window == first_windows[n]
+            if first:
+                column_accs[n] = []
                 for r in range(O_TILES):
-                    product(column_acc[r][:], r, codes_by_row, scales_by_row, window * WINDOW, WINDOW, window == 0, window == H // BAND - 1)
+                    column_acc = column_psum.tile([P, WINDOW], F32, name="column_acc", tag="bank")
+                    column_accs[n].append(column_acc)
+            for r in range(O_TILES):
+                product(column_accs[n][r][:], r, codes_by_row, scales_by_row, window * WINDOW, WINDOW,
+                        first, window == last_windows[n])
 
         def column_sums(n):
-            sums, column_acc = pooling[n]
             for r in range(O_TILES):
                 nc.vector.tensor_reduce(
-                    out=sums[:, r, H : H + W],
-                    in_=column_acc[r][:].rearrange("p (i j) -> p j i", i=BAND),
+                    out=sums[n][:, r, H : H + W],
+                    in_=column_accs[n][r][:].rearrange("p (i j) -> p j i", i=BAND),
                     axis=X_AXIS,
                     op=ADD,
                 )
 
-        def row_passes(k):
+        def row_passes(k, r, first_strip, end_strip):
             n, first_row, rows = blocks[k]
+            strips = rows * W // WINDOW
+            if first_strip == 0 and r == 0:
+                row_accs[k] = []
+            if first_strip == 0 and r % 2 == 0:
+                row_acc = row_psum.tile([P, 2, WINDOW], F32, name="row_acc", tag="bank")
+                row_accs[k].append(row_acc)
             codes_by_strip, scales_by_strip = quantised[n][2:4]
-            width = row_window(k)
-            strips = rows * W // width
-            if k in second_of:
-                row_accs[k] = row_accs[second_of[k]]
-            else:
-                row_accs[k] = [psum.tile([P, WIDE], F32, name="row_acc", tag="bank") for r in range(O_TILES)]
-            first_column = WINDOW if k in second_of else 0
-            for r in range(O_TILES):
-                for s in range(strips):
-                    product(row_accs[k][r][:, first_column : first_column + width], r, codes_by_strip, scales_by_strip,
-                            first_row * W + s * width, width, s == 0, s == strips - 1)
+            for s in range(first_strip, end_strip):
+                product(row_accs[k][r // 2][:, r % 2, :], r, codes_by_strip, scales_by_strip,
+                        first_row * W + s * WINDOW, WINDOW, s == 0, s == strips - 1)
 
-        def row_sums(k, r):
+        def row_sums(k, first_tile, tiles):
             n, first_row, rows = blocks[k]
-            strip = row_window(k) // rows
-            if k + 1 in second_of:
-                rows = 2 * rows
             nc.vector.tensor_reduce(
-                out=pooling[n][0][:, r, first_row : first_row + rows],
-                in_=row_accs[k][r][:, 0 : rows * strip].rearrange("p (i j) -> p i j", j=strip),
+                out=sums[n][:, first_tile : first_tile + tiles, first_row : first_row + rows],
+                in_=row_accs[k][first_tile // 2][:, first_tile % 2 : first_tile % 2 + tiles, :].rearrange("p r (i j) -> p r i j", i=rows),
                 axis=X_AXIS,
                 op=ADD,
             )
 
-        def finish(n, r):
+        def once(n, first_row, r):
+            codes_by_row, scales_by_row = quantised[n][0:2]
+            acc = once_psum.tile([P, PIECE_PIXELS], F32, name="once_acc", tag="bank")
+            product(acc[:], r, codes_by_row, scales_by_row, first_row * W, PIECE_PIXELS, True, True)
+            once_accs[(n, first_row, r)] = acc
+
+        def once_reads(n, first_row, r):
+            acc = once_accs[(n, first_row, r)]
+            nc.vector.tensor_reduce(
+                out=sums[n][:, r, first_row : first_row + PIECE_ROWS],
+                in_=acc[:].rearrange("p (i j) -> p i j", j=W),
+                axis=X_AXIS,
+                op=ADD,
+            )
+            nc.vector.tensor_reduce(
+                out=once_columns[n][:, r, once_pieces[n].index(first_row), :],
+                in_=acc[:].rearrange("p (i j) -> p j i", j=W),
+                axis=X_AXIS,
+                op=ADD,
+            )
+
+        def add_once_columns(n):
+            once_sums = const.tile([P, O_TILES, W], F32, name="once_sums%d" % n)
+            nc.vector.tensor_reduce(
+                out=once_sums[:],
+                in_=once_columns[n][:].rearrange("p r w j -> p r j w"),
+                axis=X_AXIS,
+                op=ADD,
+            )
+            nc.vector.tensor_tensor(out=sums[n][:, :, H : H + W], in0=sums[n][:, :, H : H + W], in1=once_sums[:], op=ADD)
+
+        def finish(n):
+            for r in range(O_TILES):
+                finish_tile(n, r)
+
+        def finish_tile(n, r):
             pooled_to = [out_0[n], out_1[n], out_2[n, 0:P], out_2[n, P : 2 * P]]
             pooled = small.tile([P, H + W], F32, name="pooled")
-            nc.scalar.activation(out=pooled[:], in_=pooling[n][0][:, r, :], func=IDENTITY, bias=bias[:, r : r + 1], scale=1.0 / W)
+            nc.scalar.activation(out=pooled[:], in_=sums[n][:, r, :], func=IDENTITY, bias=bias[:, r : r + 1], scale=1.0 / W)
             nc.sync.dma_start(out=pooled_to[r], in_=pooled[:])
 
+        scale_tiles = []
         for n in range(B):
             codes_by_row = keep.tile([P, PIXELS], U32, align_bytes=256, name="codes_by_row")
-            scales_by_row = keep.tile([P, PIXELS], U8, align_bytes=256, name="scales_by_row")
             codes_by_strip = keep.tile([P, PIXELS], U32, align_bytes=256, name="codes_by_strip")
             scales_by_strip = keep.tile([P, PIXELS], U8, align_bytes=256, name="scales_by_strip")
+            image_sums = keep.tile([P, O_TILES, H + W], F32, name="sums")
+            if SCALE_TILES[n] == len(scale_tiles):
+                scales_by_row = const.tile([P, PIXELS], U8, align_bytes=256, name="scales_by_row%d" % n)
+                (nc.vector if n < 2 else nc.gpsimd).memset(scales_by_row[:].bitcast(I32), 0)
+                scale_tiles.append(scales_by_row)
+            scales_by_row = scale_tiles[SCALE_TILES[n]]
             quantised[n] = (codes_by_row, scales_by_row, codes_by_strip, scales_by_strip)
-
-        def clear_scales(n):
-            nc.vector.memset(quantised[n][1][:].bitcast(I32), 0)
-
-        clear_scales(0)
-        clear_scales(1)
+            sums[n] = image_sums
+        once_accs = {}
+        once_columns = {}
+        once_pieces = {}
+        for n in range(B):
+            once_pieces[n] = [first_row for m, first_row, rows, k in pieces if m == n and k is None]
+            if once_pieces[n]:
+                columns = const.tile([P, O_TILES, len(once_pieces[n]), W], F32, name="once_columns%d" % n)
+                once_columns[n] = columns
 
         bias_rows = const.tile([P, P], BF16)
         nc.gpsimd.memset(bias_rows[:], 0.0)
@@ -221,14 +263,13 @@ def tile_pam_module_pa_t_kernel(tc, x, Wq, bq, Wk, bk, Wv, bv, out_0, out_1, out
         w_rows = const.tile([P, O_TILES * C], BF16)
         nc.sync.dma_start(out=w_rows[:, 0:C], in_=Wq)
         nc.sync.dma_start(out=w_rows[:, C : 2 * C], in_=Wk)
-        sequence = [(k, index) for k in range(K) for index in range(len(pieces(k)))]
-        load_piece(*sequence[0])
+        load(0)
         nc.sync.dma_start(
             out=w_rows[:, 2 * C : 4 * C].rearrange("o (r c) -> o r c", r=2),
             in_=Wv.rearrange("(r o) c -> o r c", r=2),
         )
-        for step in range(1, LOADS_AHEAD):
-            load_piece(*sequence[step])
+        for piece in range(1, LOADS_AHEAD):
+            load(piece)
 
         w_pairs = w_rows[:].bitcast(F32).rearrange("o (r p u) -> o r u p", r=O_TILES, u=2)
         w_grouped = const.tile([P, O_TILES * P * PACK], BF16, align_bytes=64)
@@ -237,7 +278,7 @@ def tile_pam_module_pa_t_kernel(tc, x, Wq, bq, Wk, bk, Wv, bv, out_0, out_1, out
         w_scales = const.tile([P, O_TILES * W_SLOT], U8, align_bytes=256)
         turned_halves = []
         for half in range(2):
-            turned = psum.tile([P, 2, 2, P], F32, name="turned", tag="bank")
+            turned = row_psum.tile([P, 2, 2, P], F32, name="turned", tag="bank")
             for r in range(2):
                 for u in range(2):
                     nc.tensor.transpose(turned[:, r, u, :], w_pairs[:, 2 * half + r, u, :], identity[:])
@@ -258,59 +299,99 @@ def tile_pam_module_pa_t_kernel(tc, x, Wq, bq, Wk, bk, Wv, bv, out_0, out_1, out
                 )
 
         weights_out(0)
-        regroup(*sequence[0])
-        regroup(*sequence[1])
+        for piece in range(REGROUP_AHEAD):
+            regroup(piece)
         weights_quantise(0)
-        quantise(*sequence[0])
+        quantise(0)
         weights_out(1)
         weights_quantise(1)
 
-        strips_done = 0
-        rows_in_psum = []
-        to_finish = []
-        for step in range(len(sequence)):
-            k, index = sequence[step]
-            n, first_row, rows = blocks[k]
-            last_piece = index == len(pieces(k)) - 1
-            if step + LOADS_AHEAD < len(sequence):
-                load_piece(*sequence[step + LOADS_AHEAD])
-            piece_end = pieces(k)[index][0] + pieces(k)[index][1]
-            if last_piece or (index + 1) % STRIP_PIECES == 0:
-                to_strips(k, strips_done, piece_end)
-                strips_done = 0 if last_piece else piece_end
-            if step + 2 < len(sequence):
-                regroup(*sequence[step + 2])
-            if 1 <= n < B - 1 and first_row + pieces(k)[index][0] == H // 2:
-                clear_scales(n + 1)
-            if step + 1 < len(sequence):
-                quantise(*sequence[step + 1])
-            if last_piece and k not in second_of:
-                for earlier in rows_in_psum:
-                    for r in range(O_TILES):
-                        row_sums(earlier, r)
-                    if blocks[earlier][1] + blocks[earlier][2] * (2 if earlier + 1 in second_of else 1) == H:
-                        to_finish.append((step + FINISH_DELAY, blocks[earlier][0]))
-                rows_in_psum.clear()
-            column_passes(k, index)
-            if last_piece:
-                if first_row + rows == H:
-                    column_sums(n)
+        bias = const.tile([P, O_TILES], F32)
+
+        def turn_biases():
+            bias_turned = once_psum.tile([P, P], F32, name="bias_turned", tag="bank")
+            nc.tensor.transpose(bias_turned[:], bias_rows_f32[:], identity[:])
+            nc.vector.tensor_copy(out=bias[:], in_=bias_turned[:, 0:O_TILES])
+
+        twice_units = []
+        once_units = []
+        for piece in range(len(pieces)):
+            n, first_row, rows, k = pieces[piece]
+            if k is None:
+                for r in range(O_TILES):
+                    once_units.append((piece, 1.0, [(once, n, first_row, r)], [(once_reads, n, first_row, r)]))
+                if first_row == once_pieces[n][-1]:
+                    once_units[-1][3].append((add_once_columns, n))
+                    once_units[-1][3].append((finish, n))
+                continue
+            end_row = first_row + rows
+            for window in range(first_row // BAND, end_row // BAND):
+                twice_units.append((piece, 2.0, [(column_passes, n, window)], []))
+            if blocks[k][1] + blocks[k][2] == end_row:
+                if k == last_blocks[n]:
+                    twice_units[-1][3].append((column_sums, n))
                 if k == 0:
-                    bias_turned = psum.tile([P, P], F32, name="bias_turned", tag="bank")
-                    nc.tensor.transpose(bias_turned[:], bias_rows_f32[:], identity[:])
-                    bias = const.tile([P, O_TILES], F32)
-                    nc.vector.tensor_copy(out=bias[:], in_=bias_turned[:, 0:O_TILES])
-                row_passes(k)
-                if k not in second_of:
-                    rows_in_psum.append(k)
-            for due, image in list(to_finish):
-                if step >= due:
-                    for r in range(O_TILES):
-                        finish(image, r)
-                    to_finish.remove((due, image))
-        for due, image in to_finish:
-            for r in range(O_TILES):
-                finish(image, r)
+                    twice_units[-1][2].append((turn_biases,))
+                strips = blocks[k][2] * W // WINDOW
+                for r in range(O_TILES):
+                    for s in range(0, strips, 4):
+                        twice_units.append((piece, 2.0, [(row_passes, k, r, s, s + 4)], []))
+                    if k < K - 1 and r % 2 == 1:
+                        twice_units[-1][3].append((row_sums, k, r - 1, 2))
+                if k == last_blocks[n] and n < B - 1 and not once_pieces[n]:
+                    twice_units[-1][3].append((finish, n))
+
+        units = []
+        later = []
+        passes = 0.0
+        once_at = ONCE_FROM
+        for unit in twice_units:
+            here = [unit]
+            if once_units and passes >= once_at:
+                here.append(once_units.pop(0))
+                once_at += ONCE_EVERY
+            for piece, unit_passes, calls, reads in here:
+                due = [call for at, call in later if at <= passes]
+                later = [(at, call) for at, call in later if at > passes]
+                units.append((piece, unit_passes, due + calls))
+                for call in reads:
+                    delay = FINISH_DELAY if call[0] == finish else ONCE_DELAY if call[0] == once_reads or call[0] == add_once_columns else READ_DELAY
+                    later.append((passes + unit_passes + delay, call))
+            passes += unit[1]
+        assert not once_units
+        units.append((0, 0.0, [call for at, call in later]))
+
+        def do(calls):
+            for call in calls:
+                call[0](*call[1:])
+
+        passes_done = 0
+        rows_done = 0
+        strips_from = 0
+        for piece in range(len(pieces)):
+            n, first_row, rows, k = pieces[piece]
+            if piece + LOADS_AHEAD < len(pieces):
+                load(piece + LOADS_AHEAD)
+            if k is not None:
+                end_row = first_row + rows
+                block_end = blocks[k][1] + blocks[k][2]
+                if first_row == blocks[k][1]:
+                    strips_from = first_row
+                if end_row == block_end or end_row - strips_from == STRIP_ROWS:
+                    to_strips(k, strips_from - blocks[k][1], end_row - blocks[k][1])
+                    strips_from = end_row
+            if piece + REGROUP_AHEAD < len(pieces):
+                regroup(piece + REGROUP_AHEAD)
+            if piece + 1 < len(pieces):
+                quantise(piece + 1)
+            rows_done += rows
+            while units and units[0][0] <= piece and passes_done <= PACE_HEAD + PACE * rows_done:
+                unit = units.pop(0)
+                passes_done += unit[1]
+                do(unit[2])
+
+        for unit in units:
+            do(unit[2])
         for r in range(O_TILES):
-            row_sums(K - 1, r)
-            finish(B - 1, r)
+            row_sums(K - 1, r, 1)
+            finish_tile(B - 1, r)

@@ -228,6 +228,13 @@ def tile_pam_module_pa_t_kernel(tc, x, Wq, bq, Wk, bk, Wv, bv, out_0, out_1, out
             nc.scalar.activation(out=pooled[:], in_=sums[n][:, r, :], func=IDENTITY, bias=bias[:, r : r + 1], scale=1.0 / W)
             nc.sync.dma_start(out=pooled_to[r], in_=pooled[:])
 
+        identity = const.tile([P, P], F32)
+        masks.make_identity(nc, identity[:])
+        bias_rows = const.tile([P, P], BF16)
+        nc.vector.memset(bias_rows[:], 0.0)
+        first_used = const.tile([P, 1], F32)
+        nc.scalar.activation(out=first_used[:], in_=bias_rows[:, 0:1], func=IDENTITY)
+
         scale_tiles = []
         for n in range(B):
             codes_by_row = keep.tile([P, PIXELS], U32, align_bytes=256, name="codes_by_row")
@@ -250,13 +257,9 @@ def tile_pam_module_pa_t_kernel(tc, x, Wq, bq, Wk, bk, Wv, bv, out_0, out_1, out
                 columns = const.tile([P, O_TILES, len(once_pieces[n]), W], F32, name="once_columns%d" % n)
                 once_columns[n] = columns
 
-        bias_rows = const.tile([P, P], BF16)
-        nc.gpsimd.memset(bias_rows[:], 0.0)
         nc.scalar.dma_start(out=bias_rows[0:1, :], in_=bq.rearrange("(r o) -> r o", r=1))
         nc.scalar.dma_start(out=bias_rows[1:2, :], in_=bk.rearrange("(r o) -> r o", r=1))
         nc.scalar.dma_start(out=bias_rows[2:4, :], in_=bv.rearrange("(r o) -> r o", r=2))
-        identity = const.tile([P, P], F32)
-        masks.make_identity(nc, identity[:])
         bias_rows_f32 = const.tile([P, P], F32)
         nc.gpsimd.tensor_copy(out=bias_rows_f32[:], in_=bias_rows[:])
 

@@ -21,7 +21,7 @@ O_TILES = 4
 assert C == P * PACK and H == W
 
 WINDOW = 256
-BAND = WINDOW // W
+COLUMN_WINDOWS = (256, 512, 512, 512)
 PIECE_ROWS = 8
 PIECE_PIXELS = PIECE_ROWS * W
 FIRST_PIECE_ROWS = 4
@@ -36,6 +36,7 @@ PACE = 0.7
 PACE_HEAD = 2
 ONCE_FROM = 130
 ONCE_EVERY = 12.0
+COLUMN_DELAY = 0.0
 READ_DELAY = 12.0
 FINISH_DELAY = 18.0
 ONCE_DELAY = 2.0
@@ -69,13 +70,13 @@ def tile_pam_module_pa_t_kernel(tc, x, Wq, bq, Wk, bk, Wv, bv, out_0, out_1, out
             for row in range(band_row, band_row + band_rows, step):
                 pieces.append((n, row, step, len(blocks) - 1 if times == 2 else None))
         K = len(blocks)
-        first_windows = {}
-        last_windows = {}
+        first_rows = {}
+        end_rows = {}
         last_blocks = {}
         for k in range(K):
             n, first_row, rows = blocks[k]
-            first_windows.setdefault(n, first_row // BAND)
-            last_windows[n] = (first_row + rows) // BAND - 1
+            first_rows.setdefault(n, first_row)
+            end_rows[n] = first_row + rows
             last_blocks[n] = k
 
         x_channels = x.rearrange("n (p t) h w -> n p t (h w)", t=PACK)
@@ -144,23 +145,24 @@ def tile_pam_module_pa_t_kernel(tc, x, Wq, bq, Wk, bk, Wv, bv, out_0, out_1, out
                 stop=last,
             )
 
-        def column_passes(n, window):
+        def column_passes(n, first_row):
             codes_by_row, scales_by_row = quantised[n][0:2]
-            first = window == first_windows[n]
+            width = COLUMN_WINDOWS[n]
+            first = first_row == first_rows[n]
             if first:
                 column_accs[n] = []
                 for r in range(O_TILES):
-                    column_acc = column_psum.tile([P, WINDOW], F32, name="column_acc", tag="bank")
+                    column_acc = column_psum.tile([P, width], F32, name="column_acc", tag="bank")
                     column_accs[n].append(column_acc)
             for r in range(O_TILES):
-                product(column_accs[n][r][:], r, codes_by_row, scales_by_row, window * WINDOW, WINDOW,
-                        first, window == last_windows[n])
+                product(column_accs[n][r][:], r, codes_by_row, scales_by_row, first_row * W, width,
+                        first, first_row + width // W == end_rows[n])
 
         def column_sums(n):
             for r in range(O_TILES):
                 nc.vector.tensor_reduce(
                     out=sums[n][:, r, H : H + W],
-                    in_=column_accs[n][r][:].rearrange("p (i j) -> p j i", i=BAND),
+                    in_=column_accs[n][r][:].rearrange("p (i j) -> p j i", j=W),
                     axis=X_AXIS,
                     op=ADD,
                 )
@@ -328,8 +330,8 @@ def tile_pam_module_pa_t_kernel(tc, x, Wq, bq, Wk, bk, Wv, bv, out_0, out_1, out
                     once_units[-1][3].append((finish, n))
                 continue
             end_row = first_row + rows
-            for window in range(first_row // BAND, end_row // BAND):
-                twice_units.append((piece, 2.0, [(column_passes, n, window)], []))
+            for row in range(first_row, end_row, COLUMN_WINDOWS[n] // W):
+                twice_units.append((piece, COLUMN_WINDOWS[n] / 128, [(column_passes, n, row)], []))
             if blocks[k][1] + blocks[k][2] == end_row:
                 if k == last_blocks[n]:
                     twice_units[-1][3].append((column_sums, n))
@@ -348,9 +350,10 @@ def tile_pam_module_pa_t_kernel(tc, x, Wq, bq, Wk, bk, Wv, bv, out_0, out_1, out
         later = []
         passes = 0.0
         once_at = ONCE_FROM
+        total = sum([unit[1] for unit in twice_units])
         for unit in twice_units:
             here = [unit]
-            if once_units and passes >= once_at:
+            if once_units and (passes >= once_at or len(once_units) > (total - passes) / 2 - 4):
                 here.append(once_units.pop(0))
                 once_at += ONCE_EVERY
             for piece, unit_passes, calls, reads in here:
@@ -358,7 +361,7 @@ def tile_pam_module_pa_t_kernel(tc, x, Wq, bq, Wk, bk, Wv, bv, out_0, out_1, out
                 later = [(at, call) for at, call in later if at > passes]
                 units.append((piece, unit_passes, due + calls))
                 for call in reads:
-                    delay = FINISH_DELAY if call[0] == finish else ONCE_DELAY if call[0] == once_reads or call[0] == add_once_columns else READ_DELAY
+                    delay = FINISH_DELAY if call[0] == finish else ONCE_DELAY if call[0] == once_reads or call[0] == add_once_columns else COLUMN_DELAY if call[0] == column_sums else READ_DELAY
                     later.append((passes + unit_passes + delay, call))
             passes += unit[1]
         assert not once_units

@@ -21,6 +21,8 @@ O_TILES = 4
 assert C == P * PACK and H == W
 
 WINDOW = 256
+BANK = 512
+ROW_WINDOWS = (256, 512, 512, 512)
 COLUMN_WINDOWS = (256, 512, 512, 512)
 PIECE_ROWS = 8
 PIECE_PIXELS = PIECE_ROWS * W
@@ -31,12 +33,13 @@ STRIP_ROWS = 32
 RUN = 8
 REGROUP_AHEAD = 2
 LOADS_AHEAD = 7
-VECTOR_ROWS = ((12, 24, 40, 56), (16, 48), (16, 48), (16, 48))
-PACE = 0.7
+VECTOR_ROWS = ((12, 24, 40, 56), (16, 48), (16, 48), (16,))
+PACE = 0.78
 PACE_HEAD = 2
-ONCE_FROM = 130
+ONCE_FROM = 125
 ONCE_EVERY = 12.0
 COLUMN_DELAY = 0.0
+ROW_DELAY = 0.0
 READ_DELAY = 12.0
 FINISH_DELAY = 18.0
 ONCE_DELAY = 2.0
@@ -57,8 +60,7 @@ def tile_pam_module_pa_t_kernel(tc, x, Wq, bq, Wk, bk, Wv, bv, out_0, out_1, out
         grouped_pool = ctx.enter_context(tc.tile_pool(name="grouped", bufs=REGROUP_AHEAD + 2))
         small = ctx.enter_context(tc.tile_pool(name="small", bufs=8))
         column_psum = ctx.enter_context(tc.psum_pool(name="column_psum", bufs=O_TILES))
-        row_psum = ctx.enter_context(tc.psum_pool(name="row_psum", bufs=2))
-        once_psum = ctx.enter_context(tc.psum_pool(name="once_psum", bufs=2))
+        psum = ctx.enter_context(tc.psum_pool(name="psum", bufs=8 - O_TILES))
         ctx.enter_context(tc.manual_schedule())
 
         pieces = []
@@ -121,7 +123,7 @@ def tile_pam_module_pa_t_kernel(tc, x, Wq, bq, Wk, bk, Wv, bv, out_0, out_1, out
         def to_strips(k, from_row, to_row):
             n, first_row, rows = blocks[k]
             codes_by_row, scales_by_row, codes_by_strip, scales_by_strip = quantised[n]
-            strip = WINDOW // rows
+            strip = ROW_WINDOWS[n] // rows
             strips = W // strip
             pixels = slice(first_row * W, (first_row + rows) * W)
             nc.vector.tensor_copy(
@@ -169,29 +171,30 @@ def tile_pam_module_pa_t_kernel(tc, x, Wq, bq, Wk, bk, Wv, bv, out_0, out_1, out
 
         def row_passes(k, r, first_strip, end_strip):
             n, first_row, rows = blocks[k]
-            strips = rows * W // WINDOW
-            if first_strip == 0 and r == 0:
-                row_accs[k] = []
-            if first_strip == 0 and r % 2 == 0:
-                row_acc = row_psum.tile([P, 2, WINDOW], F32, name="row_acc", tag="bank")
-                row_accs[k].append(row_acc)
+            width = ROW_WINDOWS[n]
+            per_bank = BANK // width
+            strips = rows * W // width
+            if first_strip == 0 and r % per_bank == 0:
+                row_acc = psum.tile([P, per_bank, width], F32, name="row_acc", tag="bank")
+                row_accs.setdefault(k, []).append(row_acc)
             codes_by_strip, scales_by_strip = quantised[n][2:4]
             for s in range(first_strip, end_strip):
-                product(row_accs[k][r // 2][:, r % 2, :], r, codes_by_strip, scales_by_strip,
-                        first_row * W + s * WINDOW, WINDOW, s == 0, s == strips - 1)
+                product(row_accs[k][r // per_bank][:, r % per_bank, :], r, codes_by_strip, scales_by_strip,
+                        first_row * W + s * width, width, s == 0, s == strips - 1)
 
-        def row_sums(k, first_tile, tiles):
+        def row_sums(k, bank):
             n, first_row, rows = blocks[k]
+            per_bank = BANK // ROW_WINDOWS[n]
             nc.vector.tensor_reduce(
-                out=sums[n][:, first_tile : first_tile + tiles, first_row : first_row + rows],
-                in_=row_accs[k][first_tile // 2][:, first_tile % 2 : first_tile % 2 + tiles, :].rearrange("p r (i j) -> p r i j", i=rows),
+                out=sums[n][:, bank * per_bank : (bank + 1) * per_bank, first_row : first_row + rows],
+                in_=row_accs[k][bank][:].rearrange("p r (i j) -> p r i j", i=rows),
                 axis=X_AXIS,
                 op=ADD,
             )
 
         def once(n, first_row, r):
             codes_by_row, scales_by_row = quantised[n][0:2]
-            acc = once_psum.tile([P, PIECE_PIXELS], F32, name="once_acc", tag="bank")
+            acc = psum.tile([P, PIECE_PIXELS], F32, name="once_acc", tag="bank")
             product(acc[:], r, codes_by_row, scales_by_row, first_row * W, PIECE_PIXELS, True, True)
             once_accs[(n, first_row, r)] = acc
 
@@ -283,7 +286,7 @@ def tile_pam_module_pa_t_kernel(tc, x, Wq, bq, Wk, bk, Wv, bv, out_0, out_1, out
         w_scales = const.tile([P, O_TILES * W_SLOT], U8, align_bytes=256)
         turned_halves = []
         for half in range(2):
-            turned = row_psum.tile([P, 2, 2, P], F32, name="turned", tag="bank")
+            turned = psum.tile([P, 2, 2, P], F32, name="turned", tag="bank")
             for r in range(2):
                 for u in range(2):
                     nc.tensor.transpose(turned[:, r, u, :], w_pairs[:, 2 * half + r, u, :], identity[:])
@@ -314,7 +317,7 @@ def tile_pam_module_pa_t_kernel(tc, x, Wq, bq, Wk, bk, Wv, bv, out_0, out_1, out
         bias = const.tile([P, O_TILES], F32)
 
         def turn_biases():
-            bias_turned = once_psum.tile([P, P], F32, name="bias_turned", tag="bank")
+            bias_turned = psum.tile([P, P], F32, name="bias_turned", tag="bank")
             nc.tensor.transpose(bias_turned[:], bias_rows_f32[:], identity[:])
             nc.vector.tensor_copy(out=bias[:], in_=bias_turned[:, 0:O_TILES])
 
@@ -337,12 +340,16 @@ def tile_pam_module_pa_t_kernel(tc, x, Wq, bq, Wk, bk, Wv, bv, out_0, out_1, out
                     twice_units[-1][3].append((column_sums, n))
                 if k == 0:
                     twice_units[-1][2].append((turn_biases,))
-                strips = blocks[k][2] * W // WINDOW
+                per_bank = BANK // ROW_WINDOWS[n]
+                strips = blocks[k][2] * W // ROW_WINDOWS[n]
+                step = 2 * per_bank
                 for r in range(O_TILES):
-                    for s in range(0, strips, 4):
-                        twice_units.append((piece, 2.0, [(row_passes, k, r, s, s + 4)], []))
-                    if k < K - 1 and r % 2 == 1:
-                        twice_units[-1][3].append((row_sums, k, r - 1, 2))
+                    for s in range(0, strips, step):
+                        twice_units.append((piece, step * ROW_WINDOWS[n] / BANK, [(row_passes, k, r, s, s + step)], []))
+                    if r % per_bank == per_bank - 1:
+                        twice_units[-1][3].append((row_sums, k, r // per_bank))
+                        if k == K - 1:
+                            twice_units[-1][3].extend([(finish_tile, n, rr) for rr in range(r + 1 - per_bank, r + 1)])
                 if k == last_blocks[n] and n < B - 1 and not once_pieces[n]:
                     twice_units[-1][3].append((finish, n))
 
@@ -361,7 +368,7 @@ def tile_pam_module_pa_t_kernel(tc, x, Wq, bq, Wk, bk, Wv, bv, out_0, out_1, out
                 later = [(at, call) for at, call in later if at > passes]
                 units.append((piece, unit_passes, due + calls))
                 for call in reads:
-                    delay = FINISH_DELAY if call[0] == finish else ONCE_DELAY if call[0] == once_reads or call[0] == add_once_columns else COLUMN_DELAY if call[0] == column_sums else READ_DELAY
+                    delay = 0.0 if calls[0][0] == row_passes and calls[0][1] == K - 1 else FINISH_DELAY if call[0] == finish else ONCE_DELAY if call[0] == once_reads or call[0] == add_once_columns else COLUMN_DELAY if call[0] == column_sums else ROW_DELAY if call[0] == row_sums and ROW_WINDOWS[blocks[call[1]][0]] == BANK else READ_DELAY
                     later.append((passes + unit_passes + delay, call))
             passes += unit[1]
         assert not once_units
@@ -398,6 +405,3 @@ def tile_pam_module_pa_t_kernel(tc, x, Wq, bq, Wk, bk, Wv, bv, out_0, out_1, out
 
         for unit in units:
             do(unit[2])
-        for r in range(O_TILES):
-            row_sums(K - 1, r, 1)
-            finish_tile(B - 1, r)

from contextlib import ExitStack

import concourse.masks as masks
import concourse.mybir as mybir

F32 = mybir.dt.float32
BF16 = mybir.dt.bfloat16
I32 = mybir.dt.int32
U32 = mybir.dt.uint32
U8 = mybir.dt.uint8
FP8X4 = mybir.dt.float8_e4m3fn_x4
ADD = mybir.AluOpType.add
MULT = mybir.AluOpType.mult
X_AXIS = mybir.AxisListType.X

P = 128
PACK = 4
B, C, H, W = 4, 512, 64, 64
PIXELS = H * W
O_TILES = 4
assert C == P * PACK and H == W

WINDOW = 256
BANK = 512
ROW_WINDOWS = (256, 512, 512, 512)
COLUMN_WINDOWS = (256, 512, 512, 512)
PIECE_ROWS = 8
PIECE_PIXELS = PIECE_ROWS * W
FIRST_PIECE_ROWS = 4
BANDS = ((0, 0, 16, 2), (0, 32, 32, 2), (1, 0, 64, 2), (0, 16, 16, 1), (2, 0, 64, 2), (3, 0, 64, 2))
SCALE_TILES = (0, 1, 2, 1)
STRIP_ROWS = 32
RUN = 8
REGROUP_AHEAD = 2
LOADS_AHEAD = 7
VECTOR_ROWS = ((12, 24, 40, 56), (16, 48), (16, 48), (16,))
PACE = 0.78
PACE_HEAD = 2
ONCE_FROM = 125
ONCE_EVERY = 12.0
COLUMN_DELAY = 0.0
ROW_DELAY = 0.0
READ_DELAY = 12.0
FINISH_DELAY = 18.0
ONCE_DELAY = 2.0
IDENTITY = mybir.ActivationFunctionType.Identity

W_PAD = 48
W_SLOT = 256

FLOPS = 2 * B * C * (O_TILES * P) * PIXELS


def tile_pam_module_pa_t_kernel(tc, x, Wq, bq, Wk, bk, Wv, bv, out_0, out_1, out_2):
    nc = tc.nc
    with ExitStack() as ctx:
        const = ctx.enter_context(tc.tile_pool(name="const", bufs=1))
        keep = ctx.enter_context(tc.tile_pool(name="keep", bufs=B))
        raw_pool = ctx.enter_context(tc.tile_pool(name="raw", bufs=8))
        grouped_pool = ctx.enter_context(tc.tile_pool(name="grouped", bufs=REGROUP_AHEAD + 2))
        small = ctx.enter_context(tc.tile_pool(name="small", bufs=8))
        column_psum = ctx.enter_context(tc.psum_pool(name="column_psum", bufs=O_TILES))
        psum = ctx.enter_context(tc.psum_pool(name="psum", bufs=8 - O_TILES))
        ctx.enter_context(tc.manual_schedule())

        pieces = []
        blocks = []
        for n, band_row, band_rows, times in BANDS:
            if times == 2:
                blocks.append((n, band_row, band_rows))
            step = PIECE_ROWS if len(blocks) > 1 else FIRST_PIECE_ROWS
            for row in range(band_row, band_row + band_rows, step):
                pieces.append((n, row, step, len(blocks) - 1 if times == 2 else None))
        K = len(blocks)
        first_rows = {}
        end_rows = {}
        last_blocks = {}
        for k in range(K):
            n, first_row, rows = blocks[k]
            first_rows.setdefault(n, first_row)
            end_rows[n] = first_row + rows
            last_blocks[n] = k

        x_channels = x.rearrange("n (p t) h w -> n p t (h w)", t=PACK)
        raw_pieces = {}
        grouped_pieces = {}
        quantised = {}
        sums = {}
        column_accs = {}
        row_accs = {}

        def pixels_of(piece):
            n, first_row, rows, k = pieces[piece]
            return slice(first_row * W, (first_row + rows) * W)

        def load(piece):
            n, first_row, rows, k = pieces[piece]
            raw = raw_pool.tile([P, PACK, PIECE_PIXELS], BF16, name="raw")
            nc.sync.dma_start(out=raw[:, :, 0 : rows * W], in_=x_channels[n, :, :, pixels_of(piece)])
            raw_pieces[piece] = raw

        def regroup(piece):
            n, row, rows, k = pieces[piece]
            pixels = rows * W
            grouped = grouped_pool.tile([P, PIECE_PIXELS * PACK], BF16, align_bytes=64, name="grouped")
            grouped_view = grouped[:, 0 : pixels * PACK].rearrange("p (q i t) -> p q t i", i=RUN, t=PACK)
            raw_view = raw_pieces[piece][:, :, 0:pixels].rearrange("p t (q i) -> p q t i", i=RUN)
            if row in VECTOR_ROWS[n]:
                nc.vector.tensor_copy(out=grouped_view, in_=raw_view)
            else:
                nc.scalar.copy(out=grouped_view, in_=raw_view)
            grouped_pieces[piece] = grouped

        def quantise(piece):
            n, first_row, rows, k = pieces[piece]
            codes_by_row, scales_by_row = quantised[n][0:2]
            nc.vector.quantize_mx(
                out=codes_by_row[:, pixels_of(piece)].bitcast(FP8X4),
                scales=scales_by_row[:, pixels_of(piece)],
                in_=grouped_pieces[piece][:, 0 : rows * W * PACK],
            )

        def to_strips(k, from_row, to_row):
            n, first_row, rows = blocks[k]
            codes_by_row, scales_by_row, codes_by_strip, scales_by_strip = quantised[n]
            strip = ROW_WINDOWS[n] // rows
            strips = W // strip
            pixels = slice(first_row * W, (first_row + rows) * W)
            nc.vector.tensor_copy(
                out=codes_by_strip[:, pixels].bitcast(I32).rearrange("p (s i j) -> p s i j", s=strips, j=strip)[:, :, from_row:to_row, :],
                in_=codes_by_row[:, pixels].bitcast(I32).rearrange("p (i s j) -> p s i j", s=strips, j=strip)[:, :, from_row:to_row, :],
            )
            nc.vector.tensor_copy(
                out=scales_by_strip[:, pixels].bitcast(I32).rearrange("p (s i j) -> p s i j", s=strips, j=strip // 4)[:, :, from_row:to_row, :],
                in_=scales_by_row[:, pixels].bitcast(I32).rearrange("p (i s j) -> p s i j", s=strips, j=strip // 4)[:, :, from_row:to_row, :],
            )

        def product(acc, r, codes, scales, first_pixel, width, first, last):
            pixels = slice(first_pixel, first_pixel + width)
            nc.tensor.matmul_mx(
                out=acc,
                lhsT=w_codes[:, W_PAD + r * P : W_PAD + (r + 1) * P].bitcast(FP8X4),
                lhsT_scale=w_scales[:, r * W_SLOT : r * W_SLOT + P],
                rhs=codes[:, pixels].bitcast(FP8X4),
                rhs_scale=scales[:, pixels],
                start=first,
                stop=last,
            )

        def column_passes(n, first_row):
            codes_by_row, scales_by_row = quantised[n][0:2]
            width = COLUMN_WINDOWS[n]
            first = first_row == first_rows[n]
            if first:
                column_accs[n] = []
                for r in range(O_TILES):
                    column_acc = column_psum.tile([P, width], F32, name="column_acc", tag="bank")
                    column_accs[n].append(column_acc)
            for r in range(O_TILES):
                product(column_accs[n][r][:], r, codes_by_row, scales_by_row, first_row * W, width,
                        first, first_row + width // W == end_rows[n])

        def column_sums(n):
            for r in range(O_TILES):
                nc.vector.tensor_reduce(
                    out=sums[n][:, r, H : H + W],
                    in_=column_accs[n][r][:].rearrange("p (i j) -> p j i", j=W),
                    axis=X_AXIS,
                    op=ADD,
                )

        def row_passes(k, r, first_strip, end_strip):
            n, first_row, rows = blocks[k]
            width = ROW_WINDOWS[n]
            per_bank = BANK // width
            strips = rows * W // width
            if first_strip == 0 and r % per_bank == 0:
                row_acc = psum.tile([P, per_bank, width], F32, name="row_acc", tag="bank")
                row_accs.setdefault(k, []).append(row_acc)
            codes_by_strip, scales_by_strip = quantised[n][2:4]
            for s in range(first_strip, end_strip):
                product(row_accs[k][r // per_bank][:, r % per_bank, :], r, codes_by_strip, scales_by_strip,
                        first_row * W + s * width, width, s == 0, s == strips - 1)

        def row_sums(k, bank):
            n, first_row, rows = blocks[k]
            per_bank = BANK // ROW_WINDOWS[n]
            nc.vector.tensor_reduce(
                out=sums[n][:, bank * per_bank : (bank + 1) * per_bank, first_row : first_row + rows],
                in_=row_accs[k][bank][:].rearrange("p r (i j) -> p r i j", i=rows),
                axis=X_AXIS,
                op=ADD,
            )

        def once(n, first_row, r):
            codes_by_row, scales_by_row = quantised[n][0:2]
            acc = psum.tile([P, PIECE_PIXELS], F32, name="once_acc", tag="bank")
            product(acc[:], r, codes_by_row, scales_by_row, first_row * W, PIECE_PIXELS, True, True)
            once_accs[(n, first_row, r)] = acc

        def once_reads(n, first_row, r):
            acc = once_accs[(n, first_row, r)]
            nc.vector.tensor_reduce(
                out=sums[n][:, r, first_row : first_row + PIECE_ROWS],
                in_=acc[:].rearrange("p (i j) -> p i j", j=W),
                axis=X_AXIS,
                op=ADD,
            )
            nc.vector.tensor_reduce(
                out=once_columns[n][:, r, once_pieces[n].index(first_row), :],
                in_=acc[:].rearrange("p (i j) -> p j i", j=W),
                axis=X_AXIS,
                op=ADD,
            )

        def add_once_columns(n):
            once_sums = const.tile([P, O_TILES, W], F32, name="once_sums%d" % n)
            nc.vector.tensor_reduce(
                out=once_sums[:],
                in_=once_columns[n][:].rearrange("p r w j -> p r j w"),
                axis=X_AXIS,
                op=ADD,
            )
            nc.vector.tensor_tensor(out=sums[n][:, :, H : H + W], in0=sums[n][:, :, H : H + W], in1=once_sums[:], op=ADD)

        def finish(n):
            for r in range(O_TILES):
                finish_tile(n, r)

        def finish_tile(n, r):
            pooled_to = [out_0[n], out_1[n], out_2[n, 0:P], out_2[n, P : 2 * P]]
            pooled = small.tile([P, H + W], F32, name="pooled")
            nc.scalar.activation(out=pooled[:], in_=sums[n][:, r, :], func=IDENTITY, bias=bias[:, r : r + 1], scale=1.0 / W)
            nc.sync.dma_start(out=pooled_to[r], in_=pooled[:])

        identity = const.tile([P, P], F32)
        masks.make_identity(nc, identity[:])
        bias_rows = const.tile([P, P], BF16)
        nc.vector.memset(bias_rows[:], 0.0)
        first_used = const.tile([P, 1], F32)
        nc.scalar.activation(out=first_used[:], in_=bias_rows[:, 0:1], func=IDENTITY)

        scale_tiles = []
        for n in range(B):
            codes_by_row = keep.tile([P, PIXELS], U32, align_bytes=256, name="codes_by_row")
            codes_by_strip = keep.tile([P, PIXELS], U32, align_bytes=256, name="codes_by_strip")
            scales_by_strip = keep.tile([P, PIXELS], U8, align_bytes=256, name="scales_by_strip")
            image_sums = keep.tile([P, O_TILES, H + W], F32, name="sums")
            if SCALE_TILES[n] == len(scale_tiles):
                scales_by_row = const.tile([P, PIXELS], U8, align_bytes=256, name="scales_by_row%d" % n)
                (nc.vector if n < 2 else nc.gpsimd).memset(scales_by_row[:].bitcast(I32), 0)
                scale_tiles.append(scales_by_row)
            scales_by_row = scale_tiles[SCALE_TILES[n]]
            quantised[n] = (codes_by_row, scales_by_row, codes_by_strip, scales_by_strip)
            sums[n] = image_sums
        once_accs = {}
        once_columns = {}
        once_pieces = {}
        for n in range(B):
            once_pieces[n] = [first_row for m, first_row, rows, k in pieces if m == n and k is None]
            if once_pieces[n]:
                columns = const.tile([P, O_TILES, len(once_pieces[n]), W], F32, name="once_columns%d" % n)
                once_columns[n] = columns

        nc.scalar.dma_start(out=bias_rows[0:1, :], in_=bq.rearrange("(r o) -> r o", r=1))
        nc.scalar.dma_start(out=bias_rows[1:2, :], in_=bk.rearrange("(r o) -> r o", r=1))
        nc.scalar.dma_start(out=bias_rows[2:4, :], in_=bv.rearrange("(r o) -> r o", r=2))
        bias_rows_f32 = const.tile([P, P], F32)
        nc.gpsimd.tensor_copy(out=bias_rows_f32[:], in_=bias_rows[:])

        w_rows = const.tile([P, O_TILES * C], BF16)
        nc.sync.dma_start(out=w_rows[:, 0:C], in_=Wq)
        nc.sync.dma_start(out=w_rows[:, C : 2 * C], in_=Wk)
        load(0)
        nc.sync.dma_start(
            out=w_rows[:, 2 * C : 4 * C].rearrange("o (r c) -> o r c", r=2),
            in_=Wv.rearrange("(r o) c -> o r c", r=2),
        )
        for piece in range(1, LOADS_AHEAD):
            load(piece)

        w_pairs = w_rows[:].bitcast(F32).rearrange("o (r p u) -> o r u p", r=O_TILES, u=2)
        w_grouped = const.tile([P, O_TILES * P * PACK], BF16, align_bytes=64)
        w_grouped_pairs = w_grouped[:].bitcast(F32).rearrange("p (r o u) -> p r o u", r=O_TILES, u=2)
        w_codes = const.tile([P, W_PAD + O_TILES * P], U32, align_bytes=256)
        w_scales = const.tile([P, O_TILES * W_SLOT], U8, align_bytes=256)
        turned_halves = []
        for half in range(2):
            turned = psum.tile([P, 2, 2, P], F32, name="turned", tag="bank")
            for r in range(2):
                for u in range(2):
                    nc.tensor.transpose(turned[:, r, u, :], w_pairs[:, 2 * half + r, u, :], identity[:])
            turned_halves.append(turned)

        def weights_out(half):
            nc.vector.tensor_copy(
                out=w_grouped_pairs[:, 2 * half : 2 * half + 2],
                in_=turned_halves[half][:].rearrange("p r u o -> p r o u"),
            )

        def weights_quantise(half):
            for r in range(2 * half, 2 * half + 2):
                nc.vector.quantize_mx(
                    out=w_codes[:, W_PAD + r * P : W_PAD + (r + 1) * P].bitcast(FP8X4),
                    scales=w_scales[:, r * W_SLOT : r * W_SLOT + P],
                    in_=w_grouped[:, r * P * PACK : (r + 1) * P * PACK],
                )

        weights_out(0)
        for piece in range(REGROUP_AHEAD):
            regroup(piece)
        weights_quantise(0)
        quantise(0)
        weights_out(1)
        weights_quantise(1)

        bias = const.tile([P, O_TILES], F32)

        def turn_biases():
            bias_turned = psum.tile([P, P], F32, name="bias_turned", tag="bank")
            nc.tensor.transpose(bias_turned[:], bias_rows_f32[:], identity[:])
            nc.vector.tensor_copy(out=bias[:], in_=bias_turned[:, 0:O_TILES])

        twice_units = []
        once_units = []
        for piece in range(len(pieces)):
            n, first_row, rows, k = pieces[piece]
            if k is None:
                for r in range(O_TILES):
                    once_units.append((piece, 1.0, [(once, n, first_row, r)], [(once_reads, n, first_row, r)]))
                if first_row == once_pieces[n][-1]:
                    once_units[-1][3].append((add_once_columns, n))
                    once_units[-1][3].append((finish, n))
                continue
            end_row = first_row + rows
            for row in range(first_row, end_row, COLUMN_WINDOWS[n] // W):
                twice_units.append((piece, COLUMN_WINDOWS[n] / 128, [(column_passes, n, row)], []))
            if blocks[k][1] + blocks[k][2] == end_row:
                if k == last_blocks[n]:
                    twice_units[-1][3].append((column_sums, n))
                if k == 0:
                    twice_units[-1][2].append((turn_biases,))
                per_bank = BANK // ROW_WINDOWS[n]
                strips = blocks[k][2] * W // ROW_WINDOWS[n]
                step = 2 * per_bank
                for r in range(O_TILES):
                    for s in range(0, strips, step):
                        twice_units.append((piece, step * ROW_WINDOWS[n] / BANK, [(row_passes, k, r, s, s + step)], []))
                    if r % per_bank == per_bank - 1:
                        twice_units[-1][3].append((row_sums, k, r // per_bank))
                        if k == K - 1:
                            twice_units[-1][3].extend([(finish_tile, n, rr) for rr in range(r + 1 - per_bank, r + 1)])
                if k == last_blocks[n] and n < B - 1 and not once_pieces[n]:
                    twice_units[-1][3].append((finish, n))

        units = []
        later = []
        passes = 0.0
        once_at = ONCE_FROM
        total = sum([unit[1] for unit in twice_units])
        for unit in twice_units:
            here = [unit]
            if once_units and (passes >= once_at or len(once_units) > (total - passes) / 2 - 4):
                here.append(once_units.pop(0))
                once_at += ONCE_EVERY
            for piece, unit_passes, calls, reads in here:
                due = [call for at, call in later if at <= passes]
                later = [(at, call) for at, call in later if at > passes]
                units.append((piece, unit_passes, due + calls))
                for call in reads:
                    delay = 0.0 if calls[0][0] == row_passes and calls[0][1] == K - 1 else FINISH_DELAY if call[0] == finish else ONCE_DELAY if call[0] == once_reads or call[0] == add_once_columns else COLUMN_DELAY if call[0] == column_sums else ROW_DELAY if call[0] == row_sums and ROW_WINDOWS[blocks[call[1]][0]] == BANK else READ_DELAY
                    later.append((passes + unit_passes + delay, call))
            passes += unit[1]
        assert not once_units
        units.append((0, 0.0, [call for at, call in later]))

        def do(calls):
            for call in calls:
                call[0](*call[1:])

        passes_done = 0
        rows_done = 0
        strips_from = 0
        for piece in range(len(pieces)):
            n, first_row, rows, k = pieces[piece]
            if piece + LOADS_AHEAD < len(pieces):
                load(piece + LOADS_AHEAD)
            if k is not None:
                end_row = first_row + rows
                block_end = blocks[k][1] + blocks[k][2]
                if first_row == blocks[k][1]:
                    strips_from = first_row
                if end_row == block_end or end_row - strips_from == STRIP_ROWS:
                    to_strips(k, strips_from - blocks[k][1], end_row - blocks[k][1])
                    strips_from = end_row
            if piece + REGROUP_AHEAD < len(pieces):
                regroup(piece + REGROUP_AHEAD)
            if piece + 1 < len(pieces):
                quantise(piece + 1)
            rows_done += rows
            while units and units[0][0] <= piece and passes_done <= PACE_HEAD + PACE * rows_done:
                unit = units.pop(0)
                passes_done += unit[1]
                do(unit[2])

        for unit in units:
            do(unit[2])
